import numpy as np
import ml_dtypes


def mxq(x, axis, fmt="e4m3"):
    dtype, down = {"e4m3": (ml_dtypes.float8_e4m3fn, 7), "e5m2": (ml_dtypes.float8_e5m2, 14)}[fmt]
    v = np.moveaxis(np.asarray(x, np.float32).astype(ml_dtypes.bfloat16).astype(np.float64), axis, -1)
    blocks = v.reshape(v.shape[:-1] + (-1, 32))
    amax = np.abs(blocks).max(-1, keepdims=True)
    byte = np.maximum(np.where(amax > 0, np.frexp(amax)[1] - 1 + 127, 0) - down, 1)
    scale = np.exp2(byte - 127.0)
    codes = (blocks / scale).astype(np.float32).astype(dtype).astype(np.float64)
    return np.moveaxis((codes * scale).reshape(v.shape), -1, axis)


WIDE = False


def mx_kscale(k):
    if not WIDE:
        return np.ones(k)
    levels = np.array([10, -10, 5, -5, 0])
    a = np.random.permutation(np.resize(levels, k // 512 * 4)).reshape(k // 512, 4)
    idx = np.arange(k)
    return np.exp2(a[idx // 512, idx % 128 // 32])


BF16 = ml_dtypes.bfloat16


def bf(x):
    return np.asarray(x, np.float32).astype(BF16)


def f64(x):
    return np.asarray(x).astype(np.float64)


E2M1 = np.array([0.0, 0.5, 1.0, 1.5, 2.0, 3.0, 4.0, 6.0, -0.0, -0.5, -1.0, -1.5, -2.0, -3.0, -4.0, -6.0])


def pack_weight(w, fmt):
    k, n = w.shape
    w = f64(bf(w)).reshape(k // 32, 32, n)
    amax = np.abs(w).max(1)
    if fmt == "e4m3":
        byte = np.frexp(amax)[1] - 1 + 127 - 7
    else:
        mant, ex = np.frexp(amax / 6.0)
        byte = np.where(mant > 0.5, ex, ex - 1) + 127
    byte = np.clip(np.where(amax > 0, byte, 1), 1, 254)
    scaled = (w * np.exp2(127.0 - byte)[:, None, :]).reshape(k, n).astype(np.float32)
    by_word = np.ascontiguousarray(scaled.reshape(k // 512, 128, 4, n).transpose(0, 1, 3, 2))
    if fmt == "e4m3":
        words = by_word.astype(ml_dtypes.float8_e4m3fn).view(np.uint8)
    else:
        c = by_word.astype(ml_dtypes.float4_e2m1fn).view(np.uint8) & 0xF
        words = c[..., 0::2] | (c[..., 1::2] << 4)
    return np.ascontiguousarray(words), np.ascontiguousarray(byte.astype(np.uint8).reshape(k // 512, 16, n))


def unpack_weight(words, scales, fmt):
    g, p, n, _ = words.shape
    if fmt == "e4m3":
        vals = np.ascontiguousarray(words).view(ml_dtypes.float8_e4m3fn).astype(np.float64)
    else:
        nib = np.empty((g, p, n, 4), np.uint8)
        nib[..., 0::2] = words & 0xF
        nib[..., 1::2] = words >> 4
        vals = E2M1[nib]
    vals = vals * np.repeat(np.exp2(scales.astype(np.float64) - 127.0), 8, axis=1)[..., None]
    return vals.transpose(0, 1, 3, 2).reshape(g * 512, n)

def pack4(w):
    words, scales = pack_weight(w, "e2m1")
    return words.reshape(words.shape[0], 128, -1), scales


def unpack4(words, scales):
    return unpack_weight(words.reshape(words.shape[0], 128, -1, 2), scales, "e2m1")


B, IN, OUT, R, Q, ORD = 2048, 1024, 1024, 8, 256, 3
K = R ** ORD


def setup_inputs():
    s = mx_kscale(K)[np.arange(R) * (K // R + R)]
    z = np.random.standard_normal((ORD, R, B))
    z[ORD - 1] *= s[:, None]
    g = np.random.standard_normal((Q, K)) / np.sqrt(K) / np.repeat(s, K // R)
    words, scales = pack4(np.ascontiguousarray(g.T))
    return {"z": bf(z), "G2_words": words, "G2_scales": scales}


def reference(z, G2_words, G2_scales):
    Z = f64(z)
    kron = Z[0]
    for j in range(1, ORD):
        kron = kron[None] * Z[j].reshape((R,) + (1,) * j + (B,))
    kron = kron.reshape((-1, B))
    return unpack4(G2_words, G2_scales).T @ mxq(kron, 0, "e4m3")

@@ -1,0 +1,122 @@
+from contextlib import ExitStack
+
+import concourse.mybir as mybir
+from concourse.masks import make_identity
+
+BF16 = mybir.dt.bfloat16
+F32 = mybir.dt.float32
+I32 = mybir.dt.int32
+U8 = mybir.dt.uint8
+U32 = mybir.dt.uint32
+FP8X4 = mybir.dt.float8_e4m3fn_x4
+FP4X4 = mybir.dt.float4_e2m1fn_x4
+MULT = mybir.AluOpType.mult
+
+P = 128
+RANK = 8
+K = RANK * RANK * RANK
+SAMPLES = 2048
+OUT_ROWS = 256
+N_TILES = SAMPLES // P
+ROUND_TILES = 4
+ROUND = ROUND_TILES * P
+BANK_TILES = 2
+
+FLOPS = 2 * OUT_ROWS * K * SAMPLES
+
+
+def tile_fast_tucker_taylor_pa_s_kernel(tc, z, G2_words, G2_scales, out):
+    nc = tc.nc
+    with ExitStack() as ctx:
+        keep = ctx.enter_context(tc.tile_pool(name="keep", bufs=1))
+        stage = ctx.enter_context(tc.tile_pool(name="stage", bufs=4))
+        psum_z = ctx.enter_context(tc.psum_pool(name="psum_z", bufs=1))
+        psum_words = ctx.enter_context(tc.psum_pool(name="psum_words", bufs=4))
+        psum_out = ctx.enter_context(tc.psum_pool(name="psum_out", bufs=3))
+
+        z_rows = keep.tile([P, 3, P], BF16)
+        for g in (2, 1, 0):
+            nc.sync.dma_start(out=z_rows[:, g, :], in_=z[g].rearrange("a (j x) -> j a x", x=P))
+
+        w_words = keep.tile([P, 2 * OUT_ROWS], U8, align_bytes=64)
+        nc.sync.dma_start(out=w_words[:].bitcast(I32), in_=G2_words[0].bitcast(I32))
+        w_scales = keep.tile([P, OUT_ROWS], U8, align_bytes=64)
+        nc.vector.memset(w_scales[:].bitcast(I32), 0)
+        for quad in range(4):
+            nc.sync.dma_start(
+                out=w_scales[32 * quad : 32 * quad + 4, :].bitcast(I32),
+                in_=G2_scales[0, 4 * quad : 4 * quad + 4, :].bitcast(I32),
+            )
+
+        ident_bf16 = keep.tile([P, P], BF16)
+        make_identity(nc, ident_bf16[:])
+        ident_f32 = keep.tile([P, P], F32)
+        make_identity(nc, ident_f32[:])
+
+        z_t_psum = psum_z.tile([P, 3, P], BF16)
+        for g in (2, 1, 0):
+            nc.tensor.transpose(z_t_psum[:, g, :], z_rows[:, g, :], ident_bf16[:])
+        z_t = keep.tile([P, 3, N_TILES, RANK], BF16)
+        nc.scalar.copy(
+            out=z_t[:].rearrange("x g j a -> x (g j a)"),
+            in_=z_t_psum[:].rearrange("x g q -> x (g q)"),
+        )
+
+        bc_t = keep.tile([P, N_TILES, RANK * RANK], F32)
+        kron_t = keep.tile([P, N_TILES, K], BF16)
+        grouped = keep.tile([P, SAMPLES * 4], BF16, align_bytes=64)
+        grouped_words = grouped[:].bitcast(F32).rearrange("p (n u) -> p n u", u=2)
+        codes = keep.tile([P, SAMPLES], U32, align_bytes=64)
+        scales = keep.tile([P, SAMPLES], U8, align_bytes=64)
+
+        for first_tile in range(0, N_TILES, ROUND_TILES):
+            tiles = slice(first_tile, first_tile + ROUND_TILES)
+            first_col = first_tile * P
+            cols = slice(first_col, first_col + ROUND)
+
+            nc.vector.tensor_tensor(
+                out=bc_t[:, tiles, :].rearrange("x j (c b) -> x j c b", b=RANK),
+                in0=z_t[:, 2, tiles, :].unsqueeze(3).to_broadcast([P, ROUND_TILES, RANK, RANK]),
+                in1=z_t[:, 1, tiles, :].unsqueeze(2).to_broadcast([P, ROUND_TILES, RANK, RANK]),
+                op=MULT,
+            )
+            nc.vector.tensor_tensor(
+                out=kron_t[:, tiles, :].rearrange("x j (cb a) -> x j cb a", a=RANK),
+                in0=bc_t[:, tiles, :].unsqueeze(3).to_broadcast([P, ROUND_TILES, RANK * RANK, RANK]),
+                in1=z_t[:, 0, tiles, :].unsqueeze(2).to_broadcast([P, ROUND_TILES, RANK * RANK, RANK]),
+                op=MULT,
+            )
+
+            for bank_tile in range(first_tile, first_tile + ROUND_TILES, BANK_TILES):
+                words_psum = psum_words.tile([P, BANK_TILES, 2, P], F32)
+                for i in range(BANK_TILES):
+                    kron_words = kron_t[:, bank_tile + i, :].bitcast(F32)
+                    for u in range(2):
+                        nc.tensor.transpose(words_psum[:, i, u, :], kron_words[:, u : K // 2 : 2], ident_f32[:])
+                nc.scalar.copy(
+                    out=grouped_words[:, bank_tile * P : (bank_tile + BANK_TILES) * P, :].rearrange(
+                        "p (i x) u -> p i x u", i=BANK_TILES
+                    ),
+                    in_=words_psum[:].rearrange("p i u x -> p i x u"),
+                )
+
+            nc.vector.quantize_mx(
+                out=codes[:, cols].bitcast(FP8X4),
+                scales=scales[:, cols],
+                in_=grouped[:, 4 * first_col : 4 * (first_col + ROUND)],
+            )
+
+            for m in range(OUT_ROWS // P):
+                acc = psum_out.tile([P, ROUND], F32)
+                nc.tensor.matmul_mx(
+                    out=acc[:],
+                    lhsT=w_words[:, 2 * P * m : 2 * P * (m + 1)].bitcast(FP4X4),
+                    lhsT_scale=w_scales[:, P * m : P * (m + 1)],
+                    rhs=codes[:, cols].bitcast(FP8X4),
+                    rhs_scale=scales[:, cols],
+                    start=True,
+                    stop=True,
+                )
+                result = stage.tile([P, ROUND], F32)
+                nc.scalar.copy(out=result[:], in_=acc[:])
+                nc.sync.dma_start(out=out[P * m : P * (m + 1), cols], in_=result[:])

@@ -1,7 +1,6 @@
 from contextlib import ExitStack
 
 import concourse.mybir as mybir
-from concourse.masks import make_identity
 
 BF16 = mybir.dt.bfloat16
 F32 = mybir.dt.float32
@@ -13,14 +12,12 @@ FP4X4 = mybir.dt.float4_e2m1fn_x4
 MULT = mybir.AluOpType.mult
 
 P = 128
+PACK = 4
 RANK = 8
 K = RANK * RANK * RANK
 SAMPLES = 2048
 OUT_ROWS = 256
-N_TILES = SAMPLES // P
-ROUND_TILES = 4
-ROUND = ROUND_TILES * P
-BANK_TILES = 2
+ROUND = 512
 
 FLOPS = 2 * OUT_ROWS * K * SAMPLES
 
@@ -30,82 +27,60 @@ def tile_fast_tucker_taylor_pa_s_kernel(tc, z, G2_words, G2_scales, out):
     with ExitStack() as ctx:
         keep = ctx.enter_context(tc.tile_pool(name="keep", bufs=1))
         stage = ctx.enter_context(tc.tile_pool(name="stage", bufs=4))
-        psum_z = ctx.enter_context(tc.psum_pool(name="psum_z", bufs=1))
-        psum_words = ctx.enter_context(tc.psum_pool(name="psum_words", bufs=4))
-        psum_out = ctx.enter_context(tc.psum_pool(name="psum_out", bufs=3))
+        psum_out = ctx.enter_context(tc.psum_pool(name="psum_out", bufs=4))
 
-        z_rows = keep.tile([P, 3, P], BF16)
-        for g in (2, 1, 0):
-            nc.sync.dma_start(out=z_rows[:, g, :], in_=z[g].rearrange("a (j x) -> j a x", x=P))
-
+        z0_rep = keep.tile([P, PACK, SAMPLES], BF16)
+        z1_rep = keep.tile([P, SAMPLES], BF16)
+        z2_rep = keep.tile([P, SAMPLES], BF16)
         w_words = keep.tile([P, 2 * OUT_ROWS], U8, align_bytes=64)
-        nc.sync.dma_start(out=w_words[:].bitcast(I32), in_=G2_words[0].bitcast(I32))
         w_scales = keep.tile([P, OUT_ROWS], U8, align_bytes=64)
-        nc.vector.memset(w_scales[:].bitcast(I32), 0)
-        for quad in range(4):
-            nc.sync.dma_start(
-                out=w_scales[32 * quad : 32 * quad + 4, :].bitcast(I32),
-                in_=G2_scales[0, 4 * quad : 4 * quad + 4, :].bitcast(I32),
-            )
-
-        ident_bf16 = keep.tile([P, P], BF16)
-        make_identity(nc, ident_bf16[:])
-        ident_f32 = keep.tile([P, P], F32)
-        make_identity(nc, ident_f32[:])
-
-        z_t_psum = psum_z.tile([P, 3, P], BF16)
-        for g in (2, 1, 0):
-            nc.tensor.transpose(z_t_psum[:, g, :], z_rows[:, g, :], ident_bf16[:])
-        z_t = keep.tile([P, 3, N_TILES, RANK], BF16)
-        nc.scalar.copy(
-            out=z_t[:].rearrange("x g j a -> x (g j a)"),
-            in_=z_t_psum[:].rearrange("x g q -> x (g q)"),
-        )
-
-        bc_t = keep.tile([P, N_TILES, RANK * RANK], F32)
-        kron_t = keep.tile([P, N_TILES, K], BF16)
-        grouped = keep.tile([P, SAMPLES * 4], BF16, align_bytes=64)
-        grouped_words = grouped[:].bitcast(F32).rearrange("p (n u) -> p n u", u=2)
+        bc = keep.tile([P, SAMPLES], F32)
+        grouped = keep.tile([P, SAMPLES, PACK], BF16, align_bytes=64)
         codes = keep.tile([P, SAMPLES], U32, align_bytes=64)
         scales = keep.tile([P, SAMPLES], U8, align_bytes=64)
 
-        for first_tile in range(0, N_TILES, ROUND_TILES):
-            tiles = slice(first_tile, first_tile + ROUND_TILES)
-            first_col = first_tile * P
-            cols = slice(first_col, first_col + ROUND)
-
-            nc.vector.tensor_tensor(
-                out=bc_t[:, tiles, :].rearrange("x j (c b) -> x j c b", b=RANK),
-                in0=z_t[:, 2, tiles, :].unsqueeze(3).to_broadcast([P, ROUND_TILES, RANK, RANK]),
-                in1=z_t[:, 1, tiles, :].unsqueeze(2).to_broadcast([P, ROUND_TILES, RANK, RANK]),
-                op=MULT,
+        def load_z(cols):
+            nc.sync.dma_start(
+                out=z2_rep[:, cols], in_=z[2, :, cols].unsqueeze(1).to_broadcast([RANK, 2 * RANK, ROUND])
             )
-            nc.vector.tensor_tensor(
-                out=kron_t[:, tiles, :].rearrange("x j (cb a) -> x j cb a", a=RANK),
-                in0=bc_t[:, tiles, :].unsqueeze(3).to_broadcast([P, ROUND_TILES, RANK * RANK, RANK]),
-                in1=z_t[:, 0, tiles, :].unsqueeze(2).to_broadcast([P, ROUND_TILES, RANK * RANK, RANK]),
-                op=MULT,
-            )
-
-            for bank_tile in range(first_tile, first_tile + ROUND_TILES, BANK_TILES):
-                words_psum = psum_words.tile([P, BANK_TILES, 2, P], F32)
-                for i in range(BANK_TILES):
-                    kron_words = kron_t[:, bank_tile + i, :].bitcast(F32)
-                    for u in range(2):
-                        nc.tensor.transpose(words_psum[:, i, u, :], kron_words[:, u : K // 2 : 2], ident_f32[:])
-                nc.scalar.copy(
-                    out=grouped_words[:, bank_tile * P : (bank_tile + BANK_TILES) * P, :].rearrange(
-                        "p (i x) u -> p i x u", i=BANK_TILES
-                    ),
-                    in_=words_psum[:].rearrange("p i u x -> p i x u"),
+            for h in range(2):
+                nc.sync.dma_start(
+                    out=z1_rep[h:P:2, cols], in_=z[1, :, cols].unsqueeze(0).to_broadcast([RANK, RANK, ROUND])
+                )
+            for h in range(2):
+                nc.sync.dma_start(
+                    out=z0_rep[h:P:2, :, cols],
+                    in_=z[0, PACK * h : PACK * (h + 1), cols].unsqueeze(0).to_broadcast([P // 2, PACK, ROUND]),
                 )
 
+        def load_weights():
+            nc.sync.dma_start(out=w_words[:].bitcast(I32), in_=G2_words[0].bitcast(I32))
+            nc.vector.memset(w_scales[:].bitcast(I32), 0)
+            for quad in range(4):
+                nc.sync.dma_start(
+                    out=w_scales[32 * quad : 32 * quad + 4, :].bitcast(I32),
+                    in_=G2_scales[0, 4 * quad : 4 * quad + 4, :].bitcast(I32),
+                )
+
+        load_z(slice(0, ROUND))
+        load_weights()
+        for first_col in range(ROUND, SAMPLES, ROUND):
+            load_z(slice(first_col, first_col + ROUND))
+
+        for first_col in range(0, SAMPLES, ROUND):
+            cols = slice(first_col, first_col + ROUND)
+            nc.vector.tensor_tensor(out=bc[:, cols], in0=z1_rep[:, cols], in1=z2_rep[:, cols], op=MULT)
+            nc.vector.tensor_tensor(
+                out=grouped[:, cols, :],
+                in0=z0_rep[:, :, cols].rearrange("p t n -> p n t"),
+                in1=bc[:, cols].unsqueeze(2).to_broadcast([P, ROUND, PACK]),
+                op=MULT,
+            )
             nc.vector.quantize_mx(
                 out=codes[:, cols].bitcast(FP8X4),
                 scales=scales[:, cols],
-                in_=grouped[:, 4 * first_col : 4 * (first_col + ROUND)],
+                in_=grouped[:, cols, :].rearrange("p n t -> p (n t)"),
             )
-
             for m in range(OUT_ROWS // P):
                 acc = psum_out.tile([P, ROUND], F32)
                 nc.tensor.matmul_mx(

@@ -1,6 +1,7 @@
 from contextlib import ExitStack
 
 import concourse.mybir as mybir
+from concourse.masks import make_identity
 
 BF16 = mybir.dt.bfloat16
 F32 = mybir.dt.float32
@@ -12,12 +13,15 @@ FP4X4 = mybir.dt.float4_e2m1fn_x4
 MULT = mybir.AluOpType.mult
 
 P = 128
-PACK = 4
 RANK = 8
-K = RANK * RANK * RANK
+PAIRS = RANK * RANK
+K = RANK * PAIRS
 SAMPLES = 2048
 OUT_ROWS = 256
-ROUND = 512
+N_TILES = SAMPLES // P
+BANK_TILES = 2
+ROUND_TILES = (2, 4, 4, 4, 2)
+LAG = 2
 
 FLOPS = 2 * OUT_ROWS * K * SAMPLES
 
@@ -26,72 +30,117 @@ def tile_fast_tucker_taylor_pa_s_kernel(tc, z, G2_words, G2_scales, out):
     nc = tc.nc
     with ExitStack() as ctx:
         keep = ctx.enter_context(tc.tile_pool(name="keep", bufs=1))
+        work = ctx.enter_context(tc.tile_pool(name="work", bufs=len(ROUND_TILES)))
         stage = ctx.enter_context(tc.tile_pool(name="stage", bufs=4))
-        psum_out = ctx.enter_context(tc.psum_pool(name="psum_out", bufs=4))
+        psum_z = ctx.enter_context(tc.psum_pool(name="psum_z", bufs=1))
+        psum_words = ctx.enter_context(tc.psum_pool(name="psum_words", bufs=4))
+        psum_out = ctx.enter_context(tc.psum_pool(name="psum_out", bufs=3))
+        ctx.enter_context(tc.manual_schedule())
 
-        z0_rep = keep.tile([P, PACK, SAMPLES], BF16)
-        z1_rep = keep.tile([P, SAMPLES], BF16)
-        z2_rep = keep.tile([P, SAMPLES], BF16)
+        z_rows = keep.tile([P, 3, P], BF16)
+        nc.sync.dma_start(out=z_rows[:], in_=z.rearrange("g a (j x) -> (a j) g x", x=P))
+
         w_words = keep.tile([P, 2 * OUT_ROWS], U8, align_bytes=64)
+        nc.sync.dma_start(out=w_words[:].bitcast(I32), in_=G2_words[0].bitcast(I32))
         w_scales = keep.tile([P, OUT_ROWS], U8, align_bytes=64)
-        bc = keep.tile([P, SAMPLES], F32)
-        grouped = keep.tile([P, SAMPLES, PACK], BF16, align_bytes=64)
-        codes = keep.tile([P, SAMPLES], U32, align_bytes=64)
-        scales = keep.tile([P, SAMPLES], U8, align_bytes=64)
-
-        def load_z(cols):
+        nc.vector.memset(w_scales[:].bitcast(I32), 0)
+        for quad in range(4):
             nc.sync.dma_start(
-                out=z2_rep[:, cols], in_=z[2, :, cols].unsqueeze(1).to_broadcast([RANK, 2 * RANK, ROUND])
+                out=w_scales[32 * quad : 32 * quad + 4, :].bitcast(I32),
+                in_=G2_scales[0, 4 * quad : 4 * quad + 4, :].bitcast(I32),
             )
-            for h in range(2):
-                nc.sync.dma_start(
-                    out=z1_rep[h:P:2, cols], in_=z[1, :, cols].unsqueeze(0).to_broadcast([RANK, RANK, ROUND])
-                )
-            for h in range(2):
-                nc.sync.dma_start(
-                    out=z0_rep[h:P:2, :, cols],
-                    in_=z[0, PACK * h : PACK * (h + 1), cols].unsqueeze(0).to_broadcast([P // 2, PACK, ROUND]),
-                )
 
-        def load_weights():
-            nc.sync.dma_start(out=w_words[:].bitcast(I32), in_=G2_words[0].bitcast(I32))
-            nc.vector.memset(w_scales[:].bitcast(I32), 0)
-            for quad in range(4):
-                nc.sync.dma_start(
-                    out=w_scales[32 * quad : 32 * quad + 4, :].bitcast(I32),
-                    in_=G2_scales[0, 4 * quad : 4 * quad + 4, :].bitcast(I32),
-                )
+        ident_bf16 = keep.tile([P, P], BF16)
+        make_identity(nc, ident_bf16[:])
+        ident_f32 = keep.tile([P, P], F32)
+        make_identity(nc, ident_f32[:])
 
-        load_z(slice(0, ROUND))
-        load_weights()
-        for first_col in range(ROUND, SAMPLES, ROUND):
-            load_z(slice(first_col, first_col + ROUND))
+        z_t_psum = psum_z.tile([P, 3, P], BF16)
+        for g in (1, 2, 0):
+            nc.tensor.transpose(z_t_psum[:, g, :], z_rows[:, g, :], ident_bf16[:])
+        z12_t = keep.tile([P, 2, N_TILES, RANK], BF16)
+        nc.vector.tensor_copy(out=z12_t[:], in_=z_t_psum[:, 1:3, :].rearrange("x g (a j) -> x g j a", a=RANK))
+        z0_t = keep.tile([P, 2, N_TILES, 4], BF16)
+        for u in range(2):
+            nc.vector.tensor_copy(
+                out=z0_t[:, u, :, :].rearrange("x j (h e) -> x j h e", e=2),
+                in_=z_t_psum[:, 0, :].rearrange("x (h u e j) -> x u j h e", h=2, u=2, e=2)[:, u, :, :, :],
+            )
 
-        for first_col in range(0, SAMPLES, ROUND):
-            cols = slice(first_col, first_col + ROUND)
-            nc.vector.tensor_tensor(out=bc[:, cols], in0=z1_rep[:, cols], in1=z2_rep[:, cols], op=MULT)
+        def pair_products(first_tile, n_tiles):
+            tiles = slice(first_tile, first_tile + n_tiles)
+            bc_t = work.tile([P, n_tiles, PAIRS], F32)
             nc.vector.tensor_tensor(
-                out=grouped[:, cols, :],
-                in0=z0_rep[:, :, cols].rearrange("p t n -> p n t"),
-                in1=bc[:, cols].unsqueeze(2).to_broadcast([P, ROUND, PACK]),
+                out=bc_t[:].rearrange("x j (c b) -> x j c b", b=RANK),
+                in0=z12_t[:, 1, tiles, :].unsqueeze(3).to_broadcast([P, n_tiles, RANK, RANK]),
+                in1=z12_t[:, 0, tiles, :].unsqueeze(2).to_broadcast([P, n_tiles, RANK, RANK]),
                 op=MULT,
             )
-            nc.vector.quantize_mx(
-                out=codes[:, cols].bitcast(FP8X4),
-                scales=scales[:, cols],
-                in_=grouped[:, cols, :].rearrange("p n t -> p (n t)"),
-            )
+            return bc_t
+
+        def triple_products(bc_t, first_tile, n_tiles):
+            tiles = slice(first_tile, first_tile + n_tiles)
+            kron_t = work.tile([P, n_tiles, 2, K // 2], BF16)
+            for u in range(2):
+                nc.vector.tensor_tensor(
+                    out=kron_t[:, :, u, :].rearrange("x j (cb he) -> x j cb he", he=4),
+                    in0=bc_t[:].unsqueeze(3).to_broadcast([P, n_tiles, PAIRS, 4]),
+                    in1=z0_t[:, u, tiles, :].unsqueeze(2).to_broadcast([P, n_tiles, PAIRS, 4]),
+                    op=MULT,
+                )
+            return kron_t
+
+        def regroup(kron_t, n_tiles):
+            grouped = work.tile([P, n_tiles * P * 4], BF16, align_bytes=64)
+            grouped_words = grouped[:].bitcast(F32).rearrange("p (j x u) -> p j x u", x=P, u=2)
+            for bank_tile in range(0, n_tiles, BANK_TILES):
+                words_psum = psum_words.tile([P, BANK_TILES, 2, P], F32)
+                for i in range(BANK_TILES):
+                    for u in range(2):
+                        nc.tensor.transpose(
+                            words_psum[:, i, u, :], kron_t[:, bank_tile + i, u, :].bitcast(F32), ident_f32[:]
+                        )
+                nc.scalar.copy(
+                    out=grouped_words[:, bank_tile : bank_tile + BANK_TILES, :, :],
+                    in_=words_psum[:].rearrange("p i u x -> p i x u"),
+                )
+            return grouped
+
+        def multiply(grouped, first_tile, n_tiles, vector_helps):
+            width = n_tiles * P
+            codes = work.tile([P, width], U32, align_bytes=64)
+            scales = work.tile([P, width], U8, align_bytes=64)
+            nc.vector.quantize_mx(out=codes[:].bitcast(FP8X4), scales=scales[:], in_=grouped[:])
             for m in range(OUT_ROWS // P):
-                acc = psum_out.tile([P, ROUND], F32)
+                acc = psum_out.tile([P, width], F32)
                 nc.tensor.matmul_mx(
                     out=acc[:],
                     lhsT=w_words[:, 2 * P * m : 2 * P * (m + 1)].bitcast(FP4X4),
                     lhsT_scale=w_scales[:, P * m : P * (m + 1)],
-                    rhs=codes[:, cols].bitcast(FP8X4),
-                    rhs_scale=scales[:, cols],
+                    rhs=codes[:].bitcast(FP8X4),
+                    rhs_scale=scales[:],
                     start=True,
                     stop=True,
                 )
-                result = stage.tile([P, ROUND], F32)
-                nc.scalar.copy(out=result[:], in_=acc[:])
-                nc.sync.dma_start(out=out[P * m : P * (m + 1), cols], in_=result[:])
+                result = stage.tile([P, width], F32)
+                if vector_helps and m == 1:
+                    nc.vector.tensor_copy(out=result[:], in_=acc[:])
+                else:
+                    nc.scalar.copy(out=result[:], in_=acc[:])
+                nc.sync.dma_start(
+                    out=out[P * m : P * (m + 1), first_tile * P : first_tile * P + width], in_=result[:]
+                )
+
+        n_rounds = len(ROUND_TILES)
+        first_tiles = [sum(ROUND_TILES[:r]) for r in range(n_rounds)]
+        bc_tiles = [pair_products(first_tiles[0], ROUND_TILES[0])]
+        grouped_tiles = []
+        for step in range(n_rounds + LAG):
+            if step + 1 < n_rounds:
+                bc_tiles.append(pair_products(first_tiles[step + 1], ROUND_TILES[step + 1]))
+            if step < n_rounds:
+                kron_t = triple_products(bc_tiles[step], first_tiles[step], ROUND_TILES[step])
+                grouped_tiles.append(regroup(kron_t, ROUND_TILES[step]))
+            if step >= LAG:
+                r = step - LAG
+                multiply(grouped_tiles[r], first_tiles[r], ROUND_TILES[r], vector_helps=step >= n_rounds - 1)

@@ -21,6 +21,7 @@ OUT_ROWS = 256
 N_TILES = SAMPLES // P
 BANK_TILES = 2
 ROUND_TILES = (2, 4, 4, 4, 2)
+GPSIMD_ROUND = 2
 LAG = 2
 
 FLOPS = 2 * OUT_ROWS * K * SAMPLES
@@ -54,38 +55,41 @@ def tile_fast_tucker_taylor_pa_s_kernel(tc, z, G2_words, G2_scales, out):
         make_identity(nc, ident_bf16[:])
         ident_f32 = keep.tile([P, P], F32)
         make_identity(nc, ident_f32[:])
-
-        z_t_psum = psum_z.tile([P, 3, P], BF16)
-        for g in (1, 2, 0):
-            nc.tensor.transpose(z_t_psum[:, g, :], z_rows[:, g, :], ident_bf16[:])
-        z12_t = keep.tile([P, 2, N_TILES, RANK], BF16)
-        nc.vector.tensor_copy(out=z12_t[:], in_=z_t_psum[:, 1:3, :].rearrange("x g (a j) -> x g j a", a=RANK))
-        z0_t = keep.tile([P, 2, N_TILES, 4], BF16)
+        sort_ja = keep.tile([P, P], BF16)
+        nc.vector.tensor_copy(
+            out=sort_ja[:].rearrange("q (j a) -> q j a", a=RANK),
+            in_=ident_bf16[:].rearrange("q (a j) -> q j a", a=RANK),
+        )
+        sort_ujhe = keep.tile([P, 2, P // 2], BF16)
         for u in range(2):
             nc.vector.tensor_copy(
-                out=z0_t[:, u, :, :].rearrange("x j (h e) -> x j h e", e=2),
-                in_=z_t_psum[:, 0, :].rearrange("x (h u e j) -> x u j h e", h=2, u=2, e=2)[:, u, :, :, :],
+                out=sort_ujhe[:, u, :].rearrange("q (j h e) -> q j h e", h=2, e=2),
+                in_=ident_bf16[:].rearrange("q (h u e j) -> q u j h e", h=2, u=2, e=2)[:, u, :, :, :],
             )
 
-        def pair_products(first_tile, n_tiles):
-            tiles = slice(first_tile, first_tile + n_tiles)
+        z_t_psum = psum_z.tile([P, 3, P], BF16)
+        nc.tensor.transpose(z_t_psum[:, 1, :], z_rows[:, 1, :], sort_ja[:])
+        nc.tensor.transpose(z_t_psum[:, 2, :], z_rows[:, 2, :], sort_ja[:])
+        nc.tensor.transpose(z_t_psum[:, 0, :], z_rows[:, 0, :], sort_ujhe[:].rearrange("q u n -> q (u n)"))
+        z_t = keep.tile([P, 3, P], BF16)
+        nc.vector.tensor_copy(out=z_t[:], in_=z_t_psum[:])
+
+        def products(engine, z_near, first_tile, n_tiles):
+            rows = slice(first_tile * RANK, (first_tile + n_tiles) * RANK)
             bc_t = work.tile([P, n_tiles, PAIRS], F32)
-            nc.vector.tensor_tensor(
+            engine.tensor_tensor(
                 out=bc_t[:].rearrange("x j (c b) -> x j c b", b=RANK),
-                in0=z12_t[:, 1, tiles, :].unsqueeze(3).to_broadcast([P, n_tiles, RANK, RANK]),
-                in1=z12_t[:, 0, tiles, :].unsqueeze(2).to_broadcast([P, n_tiles, RANK, RANK]),
+                in0=z_near[:, 2, rows].rearrange("x (j c) -> x j c", c=RANK).unsqueeze(3).to_broadcast([P, n_tiles, RANK, RANK]),
+                in1=z_t[:, 1, rows].rearrange("x (j b) -> x j b", b=RANK).unsqueeze(2).to_broadcast([P, n_tiles, RANK, RANK]),
                 op=MULT,
             )
-            return bc_t
-
-        def triple_products(bc_t, first_tile, n_tiles):
-            tiles = slice(first_tile, first_tile + n_tiles)
             kron_t = work.tile([P, n_tiles, 2, K // 2], BF16)
             for u in range(2):
-                nc.vector.tensor_tensor(
+                z0_cols = slice(u * (P // 2) + first_tile * 4, u * (P // 2) + (first_tile + n_tiles) * 4)
+                engine.tensor_tensor(
                     out=kron_t[:, :, u, :].rearrange("x j (cb he) -> x j cb he", he=4),
                     in0=bc_t[:].unsqueeze(3).to_broadcast([P, n_tiles, PAIRS, 4]),
-                    in1=z0_t[:, u, tiles, :].unsqueeze(2).to_broadcast([P, n_tiles, PAIRS, 4]),
+                    in1=z_near[:, 0, z0_cols].rearrange("x (j he) -> x j he", he=4).unsqueeze(2).to_broadcast([P, n_tiles, PAIRS, 4]),
                     op=MULT,
                 )
             return kron_t
@@ -133,14 +137,13 @@ def tile_fast_tucker_taylor_pa_s_kernel(tc, z, G2_words, G2_scales, out):
 
         n_rounds = len(ROUND_TILES)
         first_tiles = [sum(ROUND_TILES[:r]) for r in range(n_rounds)]
-        bc_tiles = [pair_products(first_tiles[0], ROUND_TILES[0])]
+        gpsimd_kron_t = products(nc.gpsimd, z_t, first_tiles[GPSIMD_ROUND], ROUND_TILES[GPSIMD_ROUND])
         grouped_tiles = []
         for step in range(n_rounds + LAG):
-            if step + 1 < n_rounds:
-                bc_tiles.append(pair_products(first_tiles[step + 1], ROUND_TILES[step + 1]))
-            if step < n_rounds:
-                kron_t = triple_products(bc_tiles[step], first_tiles[step], ROUND_TILES[step])
-                grouped_tiles.append(regroup(kron_t, ROUND_TILES[step]))
+            if step < n_rounds and step != GPSIMD_ROUND:
+                kron_t = products(nc.vector, z_t_psum, first_tiles[step], ROUND_TILES[step])
             if step >= LAG:
                 r = step - LAG
                 multiply(grouped_tiles[r], first_tiles[r], ROUND_TILES[r], vector_helps=step >= n_rounds - 1)
+            if step < n_rounds:
+                grouped_tiles.append(regroup(gpsimd_kron_t if step == GPSIMD_ROUND else kron_t, ROUND_TILES[step]))

@@ -141,7 +141,7 @@ def tile_fast_tucker_taylor_pa_s_kernel(tc, z, G2_words, G2_scales, out):
         grouped_tiles = []
         for step in range(n_rounds + LAG):
             if step < n_rounds and step != GPSIMD_ROUND:
-                kron_t = products(nc.vector, z_t_psum, first_tiles[step], ROUND_TILES[step])
+                kron_t = products(nc.vector, z_t, first_tiles[step], ROUND_TILES[step])
             if step >= LAG:
                 r = step - LAG
                 multiply(grouped_tiles[r], first_tiles[r], ROUND_TILES[r], vector_helps=step >= n_rounds - 1)

@@ -13,12 +13,13 @@ FP4X4 = mybir.dt.float4_e2m1fn_x4
 MULT = mybir.AluOpType.mult
 
 P = 128
+PACK = 4
 RANK = 8
 PAIRS = RANK * RANK
+HE = RANK // 2
 K = RANK * PAIRS
 SAMPLES = 2048
 OUT_ROWS = 256
-N_TILES = SAMPLES // P
 BANK_TILES = 2
 ROUND_TILES = (2, 4, 4, 4, 2)
 GPSIMD_ROUND = 2
@@ -57,45 +58,48 @@ def tile_fast_tucker_taylor_pa_s_kernel(tc, z, G2_words, G2_scales, out):
         make_identity(nc, ident_f32[:])
         sort_ja = keep.tile([P, P], BF16)
         nc.vector.tensor_copy(
-            out=sort_ja[:].rearrange("q (j a) -> q j a", a=RANK),
-            in_=ident_bf16[:].rearrange("q (a j) -> q j a", a=RANK),
+            out=sort_ja[:].rearrange("v (j a) -> v j a", a=RANK),
+            in_=ident_bf16[:].rearrange("v (a j) -> v j a", a=RANK),
         )
         sort_ujhe = keep.tile([P, 2, P // 2], BF16)
         for u in range(2):
             nc.vector.tensor_copy(
-                out=sort_ujhe[:, u, :].rearrange("q (j h e) -> q j h e", h=2, e=2),
-                in_=ident_bf16[:].rearrange("q (h u e j) -> q u j h e", h=2, u=2, e=2)[:, u, :, :, :],
+                out=sort_ujhe[:, u, :].rearrange("v (j h e) -> v j h e", h=2, e=2),
+                in_=ident_bf16[:].rearrange("v (h u e j) -> v u j h e", h=2, u=2, e=2)[:, u, :, :, :],
             )
 
         z_t_psum = psum_z.tile([P, 3, P], BF16)
         nc.tensor.transpose(z_t_psum[:, 1, :], z_rows[:, 1, :], sort_ja[:])
         nc.tensor.transpose(z_t_psum[:, 2, :], z_rows[:, 2, :], sort_ja[:])
-        nc.tensor.transpose(z_t_psum[:, 0, :], z_rows[:, 0, :], sort_ujhe[:].rearrange("q u n -> q (u n)"))
+        nc.tensor.transpose(z_t_psum[:, 0, :], z_rows[:, 0, :], sort_ujhe[:].rearrange("v u y -> v (u y)"))
         z_t = keep.tile([P, 3, P], BF16)
         nc.vector.tensor_copy(out=z_t[:], in_=z_t_psum[:])
 
         def products(engine, z_near, first_tile, n_tiles):
             rows = slice(first_tile * RANK, (first_tile + n_tiles) * RANK)
+            z2 = z_t_psum[:, 2, rows].rearrange("x (j c) -> x j c", c=RANK)
+            z1 = z_t[:, 1, rows].rearrange("x (j b) -> x j b", b=RANK)
             bc_t = work.tile([P, n_tiles, PAIRS], F32)
-            engine.tensor_tensor(
+            nc.vector.tensor_tensor(
                 out=bc_t[:].rearrange("x j (c b) -> x j c b", b=RANK),
-                in0=z_near[:, 2, rows].rearrange("x (j c) -> x j c", c=RANK).unsqueeze(3).to_broadcast([P, n_tiles, RANK, RANK]),
-                in1=z_t[:, 1, rows].rearrange("x (j b) -> x j b", b=RANK).unsqueeze(2).to_broadcast([P, n_tiles, RANK, RANK]),
+                in0=z2.unsqueeze(3).to_broadcast([P, n_tiles, RANK, RANK]),
+                in1=z1.unsqueeze(2).to_broadcast([P, n_tiles, RANK, RANK]),
                 op=MULT,
             )
             kron_t = work.tile([P, n_tiles, 2, K // 2], BF16)
             for u in range(2):
-                z0_cols = slice(u * (P // 2) + first_tile * 4, u * (P // 2) + (first_tile + n_tiles) * 4)
+                z0_cols = slice(u * (P // 2) + first_tile * HE, u * (P // 2) + (first_tile + n_tiles) * HE)
+                z0 = z_near[:, 0, z0_cols].rearrange("x (j he) -> x j he", he=HE)
                 engine.tensor_tensor(
-                    out=kron_t[:, :, u, :].rearrange("x j (cb he) -> x j cb he", he=4),
-                    in0=bc_t[:].unsqueeze(3).to_broadcast([P, n_tiles, PAIRS, 4]),
-                    in1=z_near[:, 0, z0_cols].rearrange("x (j he) -> x j he", he=4).unsqueeze(2).to_broadcast([P, n_tiles, PAIRS, 4]),
+                    out=kron_t[:, :, u, :].rearrange("x j (cb he) -> x j cb he", he=HE),
+                    in0=bc_t[:].unsqueeze(3).to_broadcast([P, n_tiles, PAIRS, HE]),
+                    in1=z0.unsqueeze(2).to_broadcast([P, n_tiles, PAIRS, HE]),
                     op=MULT,
                 )
             return kron_t
 
         def regroup(kron_t, n_tiles):
-            grouped = work.tile([P, n_tiles * P * 4], BF16, align_bytes=64)
+            grouped = work.tile([P, n_tiles * P * PACK], BF16, align_bytes=64)
             grouped_words = grouped[:].bitcast(F32).rearrange("p (j x u) -> p j x u", x=P, u=2)
             for bank_tile in range(0, n_tiles, BANK_TILES):
                 words_psum = psum_words.tile([P, BANK_TILES, 2, P], F32)
@@ -115,24 +119,24 @@ def tile_fast_tucker_taylor_pa_s_kernel(tc, z, G2_words, G2_scales, out):
             codes = work.tile([P, width], U32, align_bytes=64)
             scales = work.tile([P, width], U8, align_bytes=64)
             nc.vector.quantize_mx(out=codes[:].bitcast(FP8X4), scales=scales[:], in_=grouped[:])
-            for m in range(OUT_ROWS // P):
+            for half in range(OUT_ROWS // P):
                 acc = psum_out.tile([P, width], F32)
                 nc.tensor.matmul_mx(
                     out=acc[:],
-                    lhsT=w_words[:, 2 * P * m : 2 * P * (m + 1)].bitcast(FP4X4),
-                    lhsT_scale=w_scales[:, P * m : P * (m + 1)],
+                    lhsT=w_words[:, 2 * P * half : 2 * P * (half + 1)].bitcast(FP4X4),
+                    lhsT_scale=w_scales[:, P * half : P * (half + 1)],
                     rhs=codes[:].bitcast(FP8X4),
                     rhs_scale=scales[:],
                     start=True,
                     stop=True,
                 )
                 result = stage.tile([P, width], F32)
-                if vector_helps and m == 1:
+                if vector_helps and half == 1:
                     nc.vector.tensor_copy(out=result[:], in_=acc[:])
                 else:
                     nc.scalar.copy(out=result[:], in_=acc[:])
                 nc.sync.dma_start(
-                    out=out[P * m : P * (m + 1), first_tile * P : first_tile * P + width], in_=result[:]
+                    out=out[P * half : P * (half + 1), first_tile * P : first_tile * P + width], in_=result[:]
                 )
 
         n_rounds = len(ROUND_TILES)
@@ -141,7 +145,7 @@ def tile_fast_tucker_taylor_pa_s_kernel(tc, z, G2_words, G2_scales, out):
         grouped_tiles = []
         for step in range(n_rounds + LAG):
             if step < n_rounds and step != GPSIMD_ROUND:
-                kron_t = products(nc.vector, z_t, first_tiles[step], ROUND_TILES[step])
+                kron_t = products(nc.vector, z_t_psum, first_tiles[step], ROUND_TILES[step])
             if step >= LAG:
                 r = step - LAG
                 multiply(grouped_tiles[r], first_tiles[r], ROUND_TILES[r], vector_helps=step >= n_rounds - 1)

@@ -15,32 +15,48 @@ MULT = mybir.AluOpType.mult
 P = 128
 PACK = 4
 RANK = 8
-PAIRS = RANK * RANK
-HE = RANK // 2
-K = RANK * PAIRS
+BH = 2 * RANK
+K = RANK * RANK * RANK
 SAMPLES = 2048
+N_TILES = SAMPLES // P
 OUT_ROWS = 256
-BANK_TILES = 2
 ROUND_TILES = (2, 4, 4, 4, 2)
 GPSIMD_ROUND = 2
-LAG = 2
+GPSIMD_PAIR_ROUNDS = (3, 4)
 
 FLOPS = 2 * OUT_ROWS * K * SAMPLES
 
 
 def tile_fast_tucker_taylor_pa_s_kernel(tc, z, G2_words, G2_scales, out):
     nc = tc.nc
+    n_rounds = len(ROUND_TILES)
+    first_tiles = [sum(ROUND_TILES[:r]) for r in range(n_rounds)]
     with ExitStack() as ctx:
         keep = ctx.enter_context(tc.tile_pool(name="keep", bufs=1))
-        work = ctx.enter_context(tc.tile_pool(name="work", bufs=len(ROUND_TILES)))
+        work = ctx.enter_context(tc.tile_pool(name="work", bufs=n_rounds))
         stage = ctx.enter_context(tc.tile_pool(name="stage", bufs=4))
         psum_z = ctx.enter_context(tc.psum_pool(name="psum_z", bufs=1))
-        psum_words = ctx.enter_context(tc.psum_pool(name="psum_words", bufs=4))
+        psum_pair = ctx.enter_context(tc.psum_pool(name="psum_pair", bufs=4))
         psum_out = ctx.enter_context(tc.psum_pool(name="psum_out", bufs=3))
         ctx.enter_context(tc.manual_schedule())
 
-        z_rows = keep.tile([P, 3, P], BF16)
-        nc.sync.dma_start(out=z_rows[:], in_=z.rearrange("g a (j x) -> (a j) g x", x=P))
+        z_rows = keep.tile([P, 2, P], BF16)
+        nc.sync.dma_start(out=z_rows[:], in_=z[1:3].rearrange("g a (j x) -> (a j) g x", x=P))
+
+        def load_a_rep(queue, r):
+            width = ROUND_TILES[r] * P
+            cols = slice(first_tiles[r] * P, first_tiles[r] * P + width)
+            a_rep = work.tile([P, PACK, width], BF16)
+            for h in range(2):
+                queue.dma_start(
+                    out=a_rep[h:P:2, :, :], in_=z[0, PACK * h : PACK * (h + 1), cols].partition_broadcast(P // 2)
+                )
+            return a_rep
+
+        a_reps = {}
+        a_reps[0] = load_a_rep(nc.sync, 0)
+        for r in (2, 1, 3, 4):
+            a_reps[r] = load_a_rep(nc.scalar, r)
 
         w_words = keep.tile([P, 2 * OUT_ROWS], U8, align_bytes=64)
         nc.sync.dma_start(out=w_words[:].bitcast(I32), in_=G2_words[0].bitcast(I32))
@@ -56,69 +72,61 @@ def tile_fast_tucker_taylor_pa_s_kernel(tc, z, G2_words, G2_scales, out):
         make_identity(nc, ident_bf16[:])
         ident_f32 = keep.tile([P, P], F32)
         make_identity(nc, ident_f32[:])
-        sort_ja = keep.tile([P, P], BF16)
-        nc.vector.tensor_copy(
-            out=sort_ja[:].rearrange("v (j a) -> v j a", a=RANK),
-            in_=ident_bf16[:].rearrange("v (a j) -> v j a", a=RANK),
+
+        acc = psum_out.tile([P, 2, P], BF16)
+        nc.tensor.transpose(acc[:, 0, :], z_rows[:, 0, :], ident_bf16[:])
+        nc.tensor.transpose(acc[:, 1, :], z_rows[:, 1, :], ident_bf16[:])
+        z2_psum = psum_z.tile([P, P], BF16)
+        nc.tensor.transpose(z2_psum[:], z_rows[:, 1, :], ident_bf16[:])
+        z1h = keep.tile([P, N_TILES, BH], BF16)
+        nc.scalar.copy(
+            out=z1h[:].rearrange("x j (b h) -> x j b h", h=2),
+            in_=acc[:, 0, :].rearrange("x (b j) -> x j b", b=RANK).unsqueeze(3).to_broadcast([P, N_TILES, RANK, 2]),
         )
-        sort_ujhe = keep.tile([P, 2, P // 2], BF16)
-        for u in range(2):
-            nc.vector.tensor_copy(
-                out=sort_ujhe[:, u, :].rearrange("v (j h e) -> v j h e", h=2, e=2),
-                in_=ident_bf16[:].rearrange("v (h u e j) -> v u j h e", h=2, u=2, e=2)[:, u, :, :, :],
-            )
+        z2_sbuf = keep.tile([P, P], BF16)
+        nc.scalar.copy(out=z2_sbuf[:], in_=acc[:, 1, :])
 
-        z_t_psum = psum_z.tile([P, 3, P], BF16)
-        nc.tensor.transpose(z_t_psum[:, 1, :], z_rows[:, 1, :], sort_ja[:])
-        nc.tensor.transpose(z_t_psum[:, 2, :], z_rows[:, 2, :], sort_ja[:])
-        nc.tensor.transpose(z_t_psum[:, 0, :], z_rows[:, 0, :], sort_ujhe[:].rearrange("v u y -> v (u y)"))
-        z_t = keep.tile([P, 3, P], BF16)
-        nc.vector.tensor_copy(out=z_t[:], in_=z_t_psum[:])
-
-        def products(engine, z_near, first_tile, n_tiles):
-            rows = slice(first_tile * RANK, (first_tile + n_tiles) * RANK)
-            z2 = z_t_psum[:, 2, rows].rearrange("x (j c) -> x j c", c=RANK)
-            z1 = z_t[:, 1, rows].rearrange("x (j b) -> x j b", b=RANK)
-            bc_t = work.tile([P, n_tiles, PAIRS], F32)
-            nc.vector.tensor_tensor(
-                out=bc_t[:].rearrange("x j (c b) -> x j c b", b=RANK),
-                in0=z2.unsqueeze(3).to_broadcast([P, n_tiles, RANK, RANK]),
-                in1=z1.unsqueeze(2).to_broadcast([P, n_tiles, RANK, RANK]),
+        def pair_products(engine, z2_near, r):
+            tiles = slice(first_tiles[r], first_tiles[r] + ROUND_TILES[r])
+            shape = [P, ROUND_TILES[r], RANK, BH]
+            pair_t = work.tile([P, ROUND_TILES[r], P], F32)
+            engine.tensor_tensor(
+                out=pair_t[:].rearrange("x j (c bh) -> x j c bh", bh=BH),
+                in0=z2_near.rearrange("x (c j) -> x j c", c=RANK)[:, tiles, :].unsqueeze(3).to_broadcast(shape),
+                in1=z1h[:, tiles, :].unsqueeze(2).to_broadcast(shape),
                 op=MULT,
             )
-            kron_t = work.tile([P, n_tiles, 2, K // 2], BF16)
-            for u in range(2):
-                z0_cols = slice(u * (P // 2) + first_tile * HE, u * (P // 2) + (first_tile + n_tiles) * HE)
-                z0 = z_near[:, 0, z0_cols].rearrange("x (j he) -> x j he", he=HE)
-                engine.tensor_tensor(
-                    out=kron_t[:, :, u, :].rearrange("x j (cb he) -> x j cb he", he=HE),
-                    in0=bc_t[:].unsqueeze(3).to_broadcast([P, n_tiles, PAIRS, HE]),
-                    in1=z0.unsqueeze(2).to_broadcast([P, n_tiles, PAIRS, HE]),
-                    op=MULT,
-                )
-            return kron_t
+            return pair_t
 
-        def regroup(kron_t, n_tiles):
-            grouped = work.tile([P, n_tiles * P * PACK], BF16, align_bytes=64)
-            grouped_words = grouped[:].bitcast(F32).rearrange("p (j x u) -> p j x u", x=P, u=2)
-            for bank_tile in range(0, n_tiles, BANK_TILES):
-                words_psum = psum_words.tile([P, BANK_TILES, 2, P], F32)
-                for i in range(BANK_TILES):
-                    for u in range(2):
-                        nc.tensor.transpose(
-                            words_psum[:, i, u, :], kron_t[:, bank_tile + i, u, :].bitcast(F32), ident_f32[:]
-                        )
-                nc.scalar.copy(
-                    out=grouped_words[:, bank_tile : bank_tile + BANK_TILES, :, :],
-                    in_=words_psum[:].rearrange("p i u x -> p i x u"),
+        def turn(pair_t, r):
+            pair = psum_pair.tile([P, ROUND_TILES[r], P], F32)
+            for i in range(ROUND_TILES[r]):
+                nc.tensor.transpose(pair[:, i, :], pair_t[:, i, :], ident_f32[:])
+            return pair
+
+        def last_products(engine, pair, r, tile_step):
+            grouped = work.tile([P, ROUND_TILES[r] * P * PACK], BF16, align_bytes=64)
+            flat = pair[:].rearrange("p i x -> p (i x)")
+            for i in range(0, ROUND_TILES[r], tile_step):
+                n = tile_step * P
+                cols = slice(i * P, i * P + n)
+                engine.tensor_tensor(
+                    out=grouped[:, PACK * i * P : PACK * (i * P + n)].rearrange("p (n t) -> p n t", t=PACK),
+                    in0=flat[:, cols].unsqueeze(2).to_broadcast([P, n, PACK]),
+                    in1=a_reps[r][:, :, cols].rearrange("p t n -> p n t"),
+                    op=MULT,
                 )
             return grouped
 
-        def multiply(grouped, first_tile, n_tiles, vector_helps):
-            width = n_tiles * P
+        def quantise(grouped, r):
+            width = ROUND_TILES[r] * P
             codes = work.tile([P, width], U32, align_bytes=64)
             scales = work.tile([P, width], U8, align_bytes=64)
             nc.vector.quantize_mx(out=codes[:].bitcast(FP8X4), scales=scales[:], in_=grouped[:])
+            return codes, scales
+
+        def multiply(codes, scales, r, vector_helps):
+            width = ROUND_TILES[r] * P
             for half in range(OUT_ROWS // P):
                 acc = psum_out.tile([P, width], F32)
                 nc.tensor.matmul_mx(
@@ -136,18 +144,34 @@ def tile_fast_tucker_taylor_pa_s_kernel(tc, z, G2_words, G2_scales, out):
                 else:
                     nc.scalar.copy(out=result[:], in_=acc[:])
                 nc.sync.dma_start(
-                    out=out[P * half : P * (half + 1), first_tile * P : first_tile * P + width], in_=result[:]
+                    out=out[P * half : P * (half + 1), first_tiles[r] * P : first_tiles[r] * P + width], in_=result[:]
                 )
 
-        n_rounds = len(ROUND_TILES)
-        first_tiles = [sum(ROUND_TILES[:r]) for r in range(n_rounds)]
-        gpsimd_kron_t = products(nc.gpsimd, z_t, first_tiles[GPSIMD_ROUND], ROUND_TILES[GPSIMD_ROUND])
-        grouped_tiles = []
-        for step in range(n_rounds + LAG):
-            if step < n_rounds and step != GPSIMD_ROUND:
-                kron_t = products(nc.vector, z_t_psum, first_tiles[step], ROUND_TILES[step])
-            if step >= LAG:
-                r = step - LAG
-                multiply(grouped_tiles[r], first_tiles[r], ROUND_TILES[r], vector_helps=step >= n_rounds - 1)
-            if step < n_rounds:
-                grouped_tiles.append(regroup(gpsimd_kron_t if step == GPSIMD_ROUND else kron_t, ROUND_TILES[step]))
+        pair_ts = {}
+        pairs = {}
+        for r in (GPSIMD_ROUND, 0, 1):
+            pair_ts[r] = pair_products(nc.vector, z2_psum[:], r)
+            pairs[r] = turn(pair_ts[r], r)
+        pair_sbuf = keep.tile([P, ROUND_TILES[GPSIMD_ROUND], P], F32)
+        nc.scalar.copy(out=pair_sbuf[:], in_=pairs[GPSIMD_ROUND][:])
+        for r in GPSIMD_PAIR_ROUNDS:
+            pair_ts[r] = pair_products(nc.gpsimd, z2_sbuf[:], r)
+            pairs[r] = turn(pair_ts[r], r)
+
+        groupeds = {}
+        groupeds[GPSIMD_ROUND] = last_products(nc.gpsimd, pair_sbuf, GPSIMD_ROUND, 1)
+        quantised = {}
+        groupeds[0] = last_products(nc.vector, pairs[0], 0, ROUND_TILES[0])
+        groupeds[1] = last_products(nc.vector, pairs[1], 1, ROUND_TILES[1])
+        quantised[0] = quantise(groupeds[0], 0)
+        multiply(quantised[0][0], quantised[0][1], 0, False)
+        groupeds[3] = last_products(nc.vector, pairs[3], 3, ROUND_TILES[3])
+        quantised[1] = quantise(groupeds[1], 1)
+        multiply(quantised[1][0], quantised[1][1], 1, False)
+        quantised[2] = quantise(groupeds[2], 2)
+        multiply(quantised[2][0], quantised[2][1], 2, False)
+        groupeds[4] = last_products(nc.vector, pairs[4], 4, ROUND_TILES[4])
+        quantised[3] = quantise(groupeds[3], 3)
+        multiply(quantised[3][0], quantised[3][1], 3, True)
+        quantised[4] = quantise(groupeds[4], 4)
+        multiply(quantised[4][0], quantised[4][1], 4, True)

@@ -21,8 +21,7 @@ SAMPLES = 2048
 N_TILES = SAMPLES // P
 OUT_ROWS = 256
 ROUND_TILES = (2, 4, 4, 4, 2)
-GPSIMD_ROUND = 2
-GPSIMD_PAIR_ROUNDS = (3, 4)
+GPSIMD_PAIR_ROUNDS = (2, 3, 4)
 
 FLOPS = 2 * OUT_ROWS * K * SAMPLES
 
@@ -55,11 +54,10 @@ def tile_fast_tucker_taylor_pa_s_kernel(tc, z, G2_words, G2_scales, out):
 
         a_reps = {}
         a_reps[0] = load_a_rep(nc.sync, 0)
-        for r in (2, 1, 3, 4):
-            a_reps[r] = load_a_rep(nc.scalar, r)
-
+        a_reps[1] = load_a_rep(nc.sync, 1)
         w_words = keep.tile([P, 2 * OUT_ROWS], U8, align_bytes=64)
         nc.sync.dma_start(out=w_words[:].bitcast(I32), in_=G2_words[0].bitcast(I32))
+        a_reps[2] = load_a_rep(nc.sync, 2)
         w_scales = keep.tile([P, OUT_ROWS], U8, align_bytes=64)
         nc.vector.memset(w_scales[:].bitcast(I32), 0)
         for quad in range(4):
@@ -67,6 +65,8 @@ def tile_fast_tucker_taylor_pa_s_kernel(tc, z, G2_words, G2_scales, out):
                 out=w_scales[32 * quad : 32 * quad + 4, :].bitcast(I32),
                 in_=G2_scales[0, 4 * quad : 4 * quad + 4, :].bitcast(I32),
             )
+        a_reps[3] = load_a_rep(nc.sync, 3)
+        a_reps[4] = load_a_rep(nc.sync, 4)
 
         ident_bf16 = keep.tile([P, P], BF16)
         make_identity(nc, ident_bf16[:])
@@ -147,31 +147,17 @@ def tile_fast_tucker_taylor_pa_s_kernel(tc, z, G2_words, G2_scales, out):
                     out=out[P * half : P * (half + 1), first_tiles[r] * P : first_tiles[r] * P + width], in_=result[:]
                 )
 
-        pair_ts = {}
         pairs = {}
-        for r in (GPSIMD_ROUND, 0, 1):
-            pair_ts[r] = pair_products(nc.vector, z2_psum[:], r)
-            pairs[r] = turn(pair_ts[r], r)
-        pair_sbuf = keep.tile([P, ROUND_TILES[GPSIMD_ROUND], P], F32)
-        nc.scalar.copy(out=pair_sbuf[:], in_=pairs[GPSIMD_ROUND][:])
-        for r in GPSIMD_PAIR_ROUNDS:
-            pair_ts[r] = pair_products(nc.gpsimd, z2_sbuf[:], r)
-            pairs[r] = turn(pair_ts[r], r)
-
         groupeds = {}
-        groupeds[GPSIMD_ROUND] = last_products(nc.gpsimd, pair_sbuf, GPSIMD_ROUND, 1)
-        quantised = {}
+        for r in range(n_rounds - 1):
+            if r in GPSIMD_PAIR_ROUNDS:
+                pairs[r] = turn(pair_products(nc.gpsimd, z2_sbuf[:], r), r)
+            else:
+                pairs[r] = turn(pair_products(nc.vector, z2_psum[:], r), r)
         groupeds[0] = last_products(nc.vector, pairs[0], 0, ROUND_TILES[0])
-        groupeds[1] = last_products(nc.vector, pairs[1], 1, ROUND_TILES[1])
-        quantised[0] = quantise(groupeds[0], 0)
-        multiply(quantised[0][0], quantised[0][1], 0, False)
-        groupeds[3] = last_products(nc.vector, pairs[3], 3, ROUND_TILES[3])
-        quantised[1] = quantise(groupeds[1], 1)
-        multiply(quantised[1][0], quantised[1][1], 1, False)
-        quantised[2] = quantise(groupeds[2], 2)
-        multiply(quantised[2][0], quantised[2][1], 2, False)
-        groupeds[4] = last_products(nc.vector, pairs[4], 4, ROUND_TILES[4])
-        quantised[3] = quantise(groupeds[3], 3)
-        multiply(quantised[3][0], quantised[3][1], 3, True)
-        quantised[4] = quantise(groupeds[4], 4)
-        multiply(quantised[4][0], quantised[4][1], 4, True)
+        pairs[n_rounds - 1] = turn(pair_products(nc.gpsimd, z2_sbuf[:], n_rounds - 1), n_rounds - 1)
+        for r in range(1, n_rounds + 1):
+            if r < n_rounds:
+                groupeds[r] = last_products(nc.vector, pairs[r], r, ROUND_TILES[r])
+            codes, scales = quantise(groupeds[r - 1], r - 1)
+            multiply(codes, scales, r - 1, r - 1 >= n_rounds - 2)

@@ -11,17 +11,21 @@ U32 = mybir.dt.uint32
 FP8X4 = mybir.dt.float8_e4m3fn_x4
 FP4X4 = mybir.dt.float4_e2m1fn_x4
 MULT = mybir.AluOpType.mult
+COPY = mybir.ActivationFunctionType.Copy
 
 P = 128
 PACK = 4
 RANK = 8
 BH = 2 * RANK
+HE = RANK // 2
 K = RANK * RANK * RANK
 SAMPLES = 2048
 N_TILES = SAMPLES // P
 OUT_ROWS = 256
+BANK_TILES = 2
 ROUND_TILES = (2, 4, 4, 4, 2)
-GPSIMD_PAIR_ROUNDS = (2, 3, 4)
+SCALAR_ROUND = 2
+GPSIMD_ROUND = 3
 
 FLOPS = 2 * OUT_ROWS * K * SAMPLES
 
@@ -35,29 +39,29 @@ def tile_fast_tucker_taylor_pa_s_kernel(tc, z, G2_words, G2_scales, out):
         work = ctx.enter_context(tc.tile_pool(name="work", bufs=n_rounds))
         stage = ctx.enter_context(tc.tile_pool(name="stage", bufs=4))
         psum_z = ctx.enter_context(tc.psum_pool(name="psum_z", bufs=1))
-        psum_pair = ctx.enter_context(tc.psum_pool(name="psum_pair", bufs=4))
+        psum_turn = ctx.enter_context(tc.psum_pool(name="psum_turn", bufs=4))
         psum_out = ctx.enter_context(tc.psum_pool(name="psum_out", bufs=3))
         ctx.enter_context(tc.manual_schedule())
 
-        z_rows = keep.tile([P, 2, P], BF16)
-        nc.sync.dma_start(out=z_rows[:], in_=z[1:3].rearrange("g a (j x) -> (a j) g x", x=P))
+        z_rows = keep.tile([P, 3, P], BF16)
+        nc.sync.dma_start(out=z_rows[:], in_=z.rearrange("g a (j x) -> (a j) g x", x=P))
 
-        def load_a_rep(queue, r):
+        def load_a_rep(r):
             width = ROUND_TILES[r] * P
             cols = slice(first_tiles[r] * P, first_tiles[r] * P + width)
             a_rep = work.tile([P, PACK, width], BF16)
             for h in range(2):
-                queue.dma_start(
+                nc.sync.dma_start(
                     out=a_rep[h:P:2, :, :], in_=z[0, PACK * h : PACK * (h + 1), cols].partition_broadcast(P // 2)
                 )
             return a_rep
 
         a_reps = {}
-        a_reps[0] = load_a_rep(nc.sync, 0)
-        a_reps[1] = load_a_rep(nc.sync, 1)
+        a_reps[0] = load_a_rep(0)
+        a_reps[GPSIMD_ROUND] = load_a_rep(GPSIMD_ROUND)
+        a_reps[1] = load_a_rep(1)
         w_words = keep.tile([P, 2 * OUT_ROWS], U8, align_bytes=64)
         nc.sync.dma_start(out=w_words[:].bitcast(I32), in_=G2_words[0].bitcast(I32))
-        a_reps[2] = load_a_rep(nc.sync, 2)
         w_scales = keep.tile([P, OUT_ROWS], U8, align_bytes=64)
         nc.vector.memset(w_scales[:].bitcast(I32), 0)
         for quad in range(4):
@@ -65,26 +69,34 @@ def tile_fast_tucker_taylor_pa_s_kernel(tc, z, G2_words, G2_scales, out):
                 out=w_scales[32 * quad : 32 * quad + 4, :].bitcast(I32),
                 in_=G2_scales[0, 4 * quad : 4 * quad + 4, :].bitcast(I32),
             )
-        a_reps[3] = load_a_rep(nc.sync, 3)
-        a_reps[4] = load_a_rep(nc.sync, 4)
+        a_reps[4] = load_a_rep(4)
 
         ident_bf16 = keep.tile([P, P], BF16)
         make_identity(nc, ident_bf16[:])
         ident_f32 = keep.tile([P, P], F32)
         make_identity(nc, ident_f32[:])
+        sort_ujhe = keep.tile([P, 2, P // 2], BF16)
+        for u in range(2):
+            nc.vector.tensor_copy(
+                out=sort_ujhe[:, u, :].rearrange("v (j h e) -> v j h e", h=2, e=2),
+                in_=ident_bf16[:].rearrange("v (h u e j) -> v u j h e", h=2, u=2, e=2)[:, u, :, :, :],
+            )
 
-        acc = psum_out.tile([P, 2, P], BF16)
-        nc.tensor.transpose(acc[:, 0, :], z_rows[:, 0, :], ident_bf16[:])
+        acc = psum_out.tile([P, 3, P], BF16)
         nc.tensor.transpose(acc[:, 1, :], z_rows[:, 1, :], ident_bf16[:])
         z2_psum = psum_z.tile([P, P], BF16)
-        nc.tensor.transpose(z2_psum[:], z_rows[:, 1, :], ident_bf16[:])
+        nc.tensor.transpose(z2_psum[:], z_rows[:, 2, :], ident_bf16[:])
+        nc.tensor.transpose(acc[:, 2, :], z_rows[:, 2, :], ident_bf16[:])
+        nc.tensor.transpose(acc[:, 0, :], z_rows[:, 0, :], sort_ujhe[:].rearrange("v u y -> v (u y)"))
         z1h = keep.tile([P, N_TILES, BH], BF16)
         nc.scalar.copy(
             out=z1h[:].rearrange("x j (b h) -> x j b h", h=2),
-            in_=acc[:, 0, :].rearrange("x (b j) -> x j b", b=RANK).unsqueeze(3).to_broadcast([P, N_TILES, RANK, 2]),
+            in_=acc[:, 1, :].rearrange("x (b j) -> x j b", b=RANK).unsqueeze(3).to_broadcast([P, N_TILES, RANK, 2]),
         )
-        z2_sbuf = keep.tile([P, P], BF16)
-        nc.scalar.copy(out=z2_sbuf[:], in_=acc[:, 1, :])
+        z0_sorted = keep.tile([P, P], BF16)
+        nc.scalar.copy(out=z0_sorted[:], in_=acc[:, 0, :])
+        z2_f32 = keep.tile([P, P], F32)
+        nc.scalar.copy(out=z2_f32[:], in_=acc[:, 2, :])
 
         def pair_products(engine, z2_near, r):
             tiles = slice(first_tiles[r], first_tiles[r] + ROUND_TILES[r])
@@ -99,10 +111,10 @@ def tile_fast_tucker_taylor_pa_s_kernel(tc, z, G2_words, G2_scales, out):
             return pair_t
 
         def turn(pair_t, r):
-            pair = psum_pair.tile([P, ROUND_TILES[r], P], F32)
+            turned = psum_turn.tile([P, ROUND_TILES[r], P], F32)
             for i in range(ROUND_TILES[r]):
-                nc.tensor.transpose(pair[:, i, :], pair_t[:, i, :], ident_f32[:])
-            return pair
+                nc.tensor.transpose(turned[:, i, :], pair_t[:, i, :], ident_f32[:])
+            return turned
 
         def last_products(engine, pair, r, tile_step):
             grouped = work.tile([P, ROUND_TILES[r] * P * PACK], BF16, align_bytes=64)
@@ -118,15 +130,52 @@ def tile_fast_tucker_taylor_pa_s_kernel(tc, z, G2_words, G2_scales, out):
                 )
             return grouped
 
-        def quantise(grouped, r):
+        def scalar_products(r):
+            n_tiles = ROUND_TILES[r]
+            tiles = slice(first_tiles[r], first_tiles[r] + n_tiles)
+            ba_t = keep.tile([P, n_tiles, 2, RANK * HE], F32)
+            z1 = z1h[:, tiles, :].rearrange("x j (b h) -> x j b h", h=2)[:, :, :, 0]
+            for u in range(2):
+                z0_cols = slice(u * (P // 2) + first_tiles[r] * HE, u * (P // 2) + (first_tiles[r] + n_tiles) * HE)
+                z0 = z0_sorted[:, z0_cols].rearrange("x (j he) -> x j he", he=HE)
+                nc.gpsimd.tensor_tensor(
+                    out=ba_t[:, :, u, :].rearrange("x j (b he) -> x j b he", he=HE),
+                    in0=z1.unsqueeze(3).to_broadcast([P, n_tiles, RANK, HE]),
+                    in1=z0.unsqueeze(2).to_broadcast([P, n_tiles, RANK, HE]),
+                    op=MULT,
+                )
+            kron_t = keep.tile([P, n_tiles, 2, K // 2], BF16)
+            for i in range(n_tiles):
+                for c in range(RANK):
+                    col = c * N_TILES + first_tiles[r] + i
+                    nc.scalar.activation(
+                        out=kron_t[:, i, :, RANK * HE * c : RANK * HE * (c + 1)],
+                        in_=ba_t[:, i, :, :],
+                        func=COPY,
+                        scale=z2_f32[:, col : col + 1],
+                    )
+            return kron_t
+
+        def regroup(kron_t, r):
+            n_tiles = ROUND_TILES[r]
+            grouped = work.tile([P, n_tiles * P * PACK], BF16, align_bytes=64)
+            grouped_words = grouped[:].bitcast(F32).rearrange("p (j x u) -> p j x u", x=P, u=2)
+            for bank_tile in range(0, n_tiles, BANK_TILES):
+                turned = psum_turn.tile([P, BANK_TILES, 2, P], F32)
+                for i in range(BANK_TILES):
+                    for u in range(2):
+                        nc.tensor.transpose(turned[:, i, u, :], kron_t[:, bank_tile + i, u, :].bitcast(F32), ident_f32[:])
+                nc.scalar.copy(
+                    out=grouped_words[:, bank_tile : bank_tile + BANK_TILES, :, :],
+                    in_=turned[:].rearrange("p i u x -> p i x u"),
+                )
+            return grouped
+
+        def multiply(grouped, r, vector_helps):
             width = ROUND_TILES[r] * P
             codes = work.tile([P, width], U32, align_bytes=64)
             scales = work.tile([P, width], U8, align_bytes=64)
             nc.vector.quantize_mx(out=codes[:].bitcast(FP8X4), scales=scales[:], in_=grouped[:])
-            return codes, scales
-
-        def multiply(codes, scales, r, vector_helps):
-            width = ROUND_TILES[r] * P
             for half in range(OUT_ROWS // P):
                 acc = psum_out.tile([P, width], F32)
                 nc.tensor.matmul_mx(
@@ -147,17 +196,22 @@ def tile_fast_tucker_taylor_pa_s_kernel(tc, z, G2_words, G2_scales, out):
                     out=out[P * half : P * (half + 1), first_tiles[r] * P : first_tiles[r] * P + width], in_=result[:]
                 )
 
-        pairs = {}
         groupeds = {}
-        for r in range(n_rounds - 1):
-            if r in GPSIMD_PAIR_ROUNDS:
-                pairs[r] = turn(pair_products(nc.gpsimd, z2_sbuf[:], r), r)
-            else:
-                pairs[r] = turn(pair_products(nc.vector, z2_psum[:], r), r)
+        pairs = {}
+        for r in (GPSIMD_ROUND, 0, 1):
+            pairs[r] = turn(pair_products(nc.vector, z2_psum[:], r), r)
+        pair_sbuf = keep.tile([P, ROUND_TILES[GPSIMD_ROUND], P], F32)
+        nc.scalar.copy(out=pair_sbuf[:], in_=pairs[GPSIMD_ROUND][:])
+        kron_t = scalar_products(SCALAR_ROUND)
+        pair_t_last = pair_products(nc.gpsimd, z2_f32[:], 4)
+        groupeds[GPSIMD_ROUND] = last_products(nc.gpsimd, pair_sbuf, GPSIMD_ROUND, 1)
         groupeds[0] = last_products(nc.vector, pairs[0], 0, ROUND_TILES[0])
-        pairs[n_rounds - 1] = turn(pair_products(nc.gpsimd, z2_sbuf[:], n_rounds - 1), n_rounds - 1)
-        for r in range(1, n_rounds + 1):
-            if r < n_rounds:
-                groupeds[r] = last_products(nc.vector, pairs[r], r, ROUND_TILES[r])
-            codes, scales = quantise(groupeds[r - 1], r - 1)
-            multiply(codes, scales, r - 1, r - 1 >= n_rounds - 2)
+        groupeds[1] = last_products(nc.vector, pairs[1], 1, ROUND_TILES[1])
+        groupeds[SCALAR_ROUND] = regroup(kron_t, SCALAR_ROUND)
+        pairs[4] = turn(pair_t_last, 4)
+        multiply(groupeds[0], 0, False)
+        groupeds[4] = last_products(nc.vector, pairs[4], 4, ROUND_TILES[4])
+        multiply(groupeds[1], 1, False)
+        multiply(groupeds[2], 2, False)
+        multiply(groupeds[3], 3, True)
+        multiply(groupeds[4], 4, True)

@@ -58,10 +58,10 @@ def tile_fast_tucker_taylor_pa_s_kernel(tc, z, G2_words, G2_scales, out):
 
         a_reps = {}
         a_reps[0] = load_a_rep(0)
-        a_reps[GPSIMD_ROUND] = load_a_rep(GPSIMD_ROUND)
         a_reps[1] = load_a_rep(1)
         w_words = keep.tile([P, 2 * OUT_ROWS], U8, align_bytes=64)
         nc.sync.dma_start(out=w_words[:].bitcast(I32), in_=G2_words[0].bitcast(I32))
+        a_reps[4] = load_a_rep(4)
         w_scales = keep.tile([P, OUT_ROWS], U8, align_bytes=64)
         nc.vector.memset(w_scales[:].bitcast(I32), 0)
         for quad in range(4):
@@ -69,7 +69,6 @@ def tile_fast_tucker_taylor_pa_s_kernel(tc, z, G2_words, G2_scales, out):
                 out=w_scales[32 * quad : 32 * quad + 4, :].bitcast(I32),
                 in_=G2_scales[0, 4 * quad : 4 * quad + 4, :].bitcast(I32),
             )
-        a_reps[4] = load_a_rep(4)
 
         ident_bf16 = keep.tile([P, P], BF16)
         make_identity(nc, ident_bf16[:])
@@ -82,94 +81,67 @@ def tile_fast_tucker_taylor_pa_s_kernel(tc, z, G2_words, G2_scales, out):
                 in_=ident_bf16[:].rearrange("v (h u e j) -> v u j h e", h=2, u=2, e=2)[:, u, :, :, :],
             )
 
-        acc = psum_out.tile([P, 3, P], BF16)
-        nc.tensor.transpose(acc[:, 1, :], z_rows[:, 1, :], ident_bf16[:])
-        z2_psum = psum_z.tile([P, P], BF16)
-        nc.tensor.transpose(z2_psum[:], z_rows[:, 2, :], ident_bf16[:])
-        nc.tensor.transpose(acc[:, 2, :], z_rows[:, 2, :], ident_bf16[:])
+        z12_psum = psum_z.tile([P, 2, P], BF16)
+        nc.tensor.transpose(z12_psum[:, 0, :], z_rows[:, 1, :], ident_bf16[:])
+        nc.tensor.transpose(z12_psum[:, 1, :], z_rows[:, 2, :], ident_bf16[:])
+        acc = psum_out.tile([P, 2, P], BF16)
         nc.tensor.transpose(acc[:, 0, :], z_rows[:, 0, :], sort_ujhe[:].rearrange("v u y -> v (u y)"))
+        nc.tensor.transpose(acc[:, 1, :], z_rows[:, 2, :], ident_bf16[:])
         z1h = keep.tile([P, N_TILES, BH], BF16)
-        nc.scalar.copy(
+        nc.vector.tensor_copy(
             out=z1h[:].rearrange("x j (b h) -> x j b h", h=2),
-            in_=acc[:, 1, :].rearrange("x (b j) -> x j b", b=RANK).unsqueeze(3).to_broadcast([P, N_TILES, RANK, 2]),
+            in_=z12_psum[:, 0, :].rearrange("x (b j) -> x j b", b=RANK).unsqueeze(3).to_broadcast([P, N_TILES, RANK, 2]),
         )
+        z2_psum = z12_psum[:, 1, :]
         z0_sorted = keep.tile([P, P], BF16)
         nc.scalar.copy(out=z0_sorted[:], in_=acc[:, 0, :])
         z2_f32 = keep.tile([P, P], F32)
-        nc.scalar.copy(out=z2_f32[:], in_=acc[:, 2, :])
+        nc.scalar.copy(out=z2_f32[:], in_=acc[:, 1, :])
 
-        def pair_products(engine, z2_near, r):
+        def z1_of(r):
+            tiles = slice(first_tiles[r], first_tiles[r] + ROUND_TILES[r])
+            return z1h[:, tiles, :].rearrange("x j (b h) -> x j b h", h=2)[:, :, :, 0]
+
+        def z0_of(r, first, n_tiles, u):
+            start = u * (P // 2) + (first_tiles[r] + first) * HE
+            return z0_sorted[:, start : start + n_tiles * HE].rearrange("x (j he) -> x j he", he=HE)
+
+        def pair_products(r):
             tiles = slice(first_tiles[r], first_tiles[r] + ROUND_TILES[r])
             shape = [P, ROUND_TILES[r], RANK, BH]
             pair_t = work.tile([P, ROUND_TILES[r], P], F32)
-            engine.tensor_tensor(
+            nc.vector.tensor_tensor(
                 out=pair_t[:].rearrange("x j (c bh) -> x j c bh", bh=BH),
-                in0=z2_near.rearrange("x (c j) -> x j c", c=RANK)[:, tiles, :].unsqueeze(3).to_broadcast(shape),
+                in0=z2_psum.rearrange("x (c j) -> x j c", c=RANK)[:, tiles, :].unsqueeze(3).to_broadcast(shape),
                 in1=z1h[:, tiles, :].unsqueeze(2).to_broadcast(shape),
                 op=MULT,
             )
-            return pair_t
-
-        def turn(pair_t, r):
             turned = psum_turn.tile([P, ROUND_TILES[r], P], F32)
             for i in range(ROUND_TILES[r]):
                 nc.tensor.transpose(turned[:, i, :], pair_t[:, i, :], ident_f32[:])
             return turned
 
-        def last_products(engine, pair, r, tile_step):
-            grouped = work.tile([P, ROUND_TILES[r] * P * PACK], BF16, align_bytes=64)
-            flat = pair[:].rearrange("p i x -> p (i x)")
-            for i in range(0, ROUND_TILES[r], tile_step):
-                n = tile_step * P
-                cols = slice(i * P, i * P + n)
-                engine.tensor_tensor(
-                    out=grouped[:, PACK * i * P : PACK * (i * P + n)].rearrange("p (n t) -> p n t", t=PACK),
-                    in0=flat[:, cols].unsqueeze(2).to_broadcast([P, n, PACK]),
-                    in1=a_reps[r][:, :, cols].rearrange("p t n -> p n t"),
-                    op=MULT,
-                )
+        def last_products(pair, r):
+            n = ROUND_TILES[r] * P
+            grouped = work.tile([P, n * PACK], BF16, align_bytes=64)
+            nc.vector.tensor_tensor(
+                out=grouped[:].rearrange("p (n t) -> p n t", t=PACK),
+                in0=pair[:].rearrange("p i x -> p (i x)").unsqueeze(2).to_broadcast([P, n, PACK]),
+                in1=a_reps[r][:].rearrange("p t n -> p n t"),
+                op=MULT,
+            )
             return grouped
 
-        def scalar_products(r):
-            n_tiles = ROUND_TILES[r]
-            tiles = slice(first_tiles[r], first_tiles[r] + n_tiles)
-            ba_t = keep.tile([P, n_tiles, 2, RANK * HE], F32)
-            z1 = z1h[:, tiles, :].rearrange("x j (b h) -> x j b h", h=2)[:, :, :, 0]
-            for u in range(2):
-                z0_cols = slice(u * (P // 2) + first_tiles[r] * HE, u * (P // 2) + (first_tiles[r] + n_tiles) * HE)
-                z0 = z0_sorted[:, z0_cols].rearrange("x (j he) -> x j he", he=HE)
-                nc.gpsimd.tensor_tensor(
-                    out=ba_t[:, :, u, :].rearrange("x j (b he) -> x j b he", he=HE),
-                    in0=z1.unsqueeze(3).to_broadcast([P, n_tiles, RANK, HE]),
-                    in1=z0.unsqueeze(2).to_broadcast([P, n_tiles, RANK, HE]),
-                    op=MULT,
-                )
-            kron_t = keep.tile([P, n_tiles, 2, K // 2], BF16)
-            for i in range(n_tiles):
-                for c in range(RANK):
-                    col = c * N_TILES + first_tiles[r] + i
-                    nc.scalar.activation(
-                        out=kron_t[:, i, :, RANK * HE * c : RANK * HE * (c + 1)],
-                        in_=ba_t[:, i, :, :],
-                        func=COPY,
-                        scale=z2_f32[:, col : col + 1],
-                    )
-            return kron_t
-
-        def regroup(kron_t, r):
-            n_tiles = ROUND_TILES[r]
-            grouped = work.tile([P, n_tiles * P * PACK], BF16, align_bytes=64)
+        def regroup(kron_t, grouped, bank_tile):
             grouped_words = grouped[:].bitcast(F32).rearrange("p (j x u) -> p j x u", x=P, u=2)
-            for bank_tile in range(0, n_tiles, BANK_TILES):
-                turned = psum_turn.tile([P, BANK_TILES, 2, P], F32)
-                for i in range(BANK_TILES):
-                    for u in range(2):
-                        nc.tensor.transpose(turned[:, i, u, :], kron_t[:, bank_tile + i, u, :].bitcast(F32), ident_f32[:])
-                nc.scalar.copy(
-                    out=grouped_words[:, bank_tile : bank_tile + BANK_TILES, :, :],
-                    in_=turned[:].rearrange("p i u x -> p i x u"),
-                )
-            return grouped
+            turned = psum_turn.tile([P, BANK_TILES, 2, P], F32)
+            for i in range(BANK_TILES):
+                for u in range(2):
+                    nc.tensor.transpose(turned[:, i, u, :], kron_t[:, bank_tile + i, u, :].bitcast(F32), ident_f32[:])
+            nc.scalar.copy(
+                out=grouped_words[:, bank_tile : bank_tile + BANK_TILES, :, :],
+                in_=turned[:].rearrange("p i u x -> p i x u"),
+            )
 
         def multiply(grouped, r, vector_helps):
             width = ROUND_TILES[r] * P
@@ -196,22 +168,71 @@ def tile_fast_tucker_taylor_pa_s_kernel(tc, z, G2_words, G2_scales, out):
                     out=out[P * half : P * (half + 1), first_tiles[r] * P : first_tiles[r] * P + width], in_=result[:]
                 )
 
-        groupeds = {}
+        S, G = SCALAR_ROUND, GPSIMD_ROUND
+        n_s, n_g = ROUND_TILES[S], ROUND_TILES[G]
         pairs = {}
-        for r in (GPSIMD_ROUND, 0, 1):
-            pairs[r] = turn(pair_products(nc.vector, z2_psum[:], r), r)
-        pair_sbuf = keep.tile([P, ROUND_TILES[GPSIMD_ROUND], P], F32)
-        nc.scalar.copy(out=pair_sbuf[:], in_=pairs[GPSIMD_ROUND][:])
-        kron_t = scalar_products(SCALAR_ROUND)
-        pair_t_last = pair_products(nc.gpsimd, z2_f32[:], 4)
-        groupeds[GPSIMD_ROUND] = last_products(nc.gpsimd, pair_sbuf, GPSIMD_ROUND, 1)
-        groupeds[0] = last_products(nc.vector, pairs[0], 0, ROUND_TILES[0])
-        groupeds[1] = last_products(nc.vector, pairs[1], 1, ROUND_TILES[1])
-        groupeds[SCALAR_ROUND] = regroup(kron_t, SCALAR_ROUND)
-        pairs[4] = turn(pair_t_last, 4)
+        groupeds = {}
+        pairs[0] = pair_products(0)
+        pairs[1] = pair_products(1)
+        pairs[4] = pair_products(4)
+
+        ba_t = keep.tile([P, n_s, 2, RANK * HE], F32)
+        for u in range(2):
+            nc.gpsimd.tensor_tensor(
+                out=ba_t[:, :, u, :].rearrange("x j (b he) -> x j b he", he=HE),
+                in0=z1_of(S).unsqueeze(3).to_broadcast([P, n_s, RANK, HE]),
+                in1=z0_of(S, 0, n_s, u).unsqueeze(2).to_broadcast([P, n_s, RANK, HE]),
+                op=MULT,
+            )
+        bc_t = keep.tile([P, n_g, RANK * RANK], F32)
+        g_tiles = slice(first_tiles[G], first_tiles[G] + n_g)
+        nc.gpsimd.tensor_tensor(
+            out=bc_t[:].rearrange("x j (c b) -> x j c b", b=RANK),
+            in0=z2_f32[:].rearrange("x (c j) -> x j c", c=RANK)[:, g_tiles, :].unsqueeze(3).to_broadcast([P, n_g, RANK, RANK]),
+            in1=z1_of(G).unsqueeze(2).to_broadcast([P, n_g, RANK, RANK]),
+            op=MULT,
+        )
+
+        kron_t_s = keep.tile([P, n_s, 2, K // 2], BF16)
+        kron_t_g = keep.tile([P, n_g, 2, K // 2], BF16)
+
+        def scalar_products(bank_tile):
+            for i in range(bank_tile, bank_tile + BANK_TILES):
+                for c in range(RANK):
+                    col = c * N_TILES + first_tiles[S] + i
+                    nc.scalar.activation(
+                        out=kron_t_s[:, i, :, RANK * HE * c : RANK * HE * (c + 1)],
+                        in_=ba_t[:, i, :, :],
+                        func=COPY,
+                        scale=z2_f32[:, col : col + 1],
+                    )
+
+        def gpsimd_products(bank_tile):
+            for u in range(2):
+                nc.gpsimd.tensor_tensor(
+                    out=kron_t_g[:, bank_tile : bank_tile + BANK_TILES, u, :].rearrange("x j (cb he) -> x j cb he", he=HE),
+                    in0=bc_t[:, bank_tile : bank_tile + BANK_TILES, :].unsqueeze(3).to_broadcast([P, BANK_TILES, RANK * RANK, HE]),
+                    in1=z0_of(G, bank_tile, BANK_TILES, u).unsqueeze(2).to_broadcast([P, BANK_TILES, RANK * RANK, HE]),
+                    op=MULT,
+                )
+
+        grouped_s = work.tile([P, n_s * P * PACK], BF16, align_bytes=64, tag="grouped")
+        grouped_g = work.tile([P, n_g * P * PACK], BF16, align_bytes=64, tag="grouped")
+        groupeds[S] = grouped_s
+        groupeds[G] = grouped_g
+        gpsimd_products(0)
+        gpsimd_products(BANK_TILES)
+        scalar_products(0)
+        scalar_products(BANK_TILES)
+        groupeds[0] = last_products(pairs[0], 0)
+        regroup(kron_t_s, grouped_s, 0)
+        regroup(kron_t_s, grouped_s, BANK_TILES)
+        groupeds[1] = last_products(pairs[1], 1)
+        groupeds[4] = last_products(pairs[4], 4)
         multiply(groupeds[0], 0, False)
-        groupeds[4] = last_products(nc.vector, pairs[4], 4, ROUND_TILES[4])
+        regroup(kron_t_g, grouped_g, 0)
         multiply(groupeds[1], 1, False)
-        multiply(groupeds[2], 2, False)
+        regroup(kron_t_g, grouped_g, BANK_TILES)
+        multiply(groupeds[2], 2, True)
         multiply(groupeds[3], 3, True)
         multiply(groupeds[4], 4, True)

@@ -39,7 +39,8 @@ def tile_fast_tucker_taylor_pa_s_kernel(tc, z, G2_words, G2_scales, out):
         work = ctx.enter_context(tc.tile_pool(name="work", bufs=n_rounds))
         stage = ctx.enter_context(tc.tile_pool(name="stage", bufs=4))
         psum_z = ctx.enter_context(tc.psum_pool(name="psum_z", bufs=1))
-        psum_turn = ctx.enter_context(tc.psum_pool(name="psum_turn", bufs=4))
+        psum_pair = ctx.enter_context(tc.psum_pool(name="psum_pair", bufs=2))
+        psum_turn = ctx.enter_context(tc.psum_pool(name="psum_turn", bufs=2))
         psum_out = ctx.enter_context(tc.psum_pool(name="psum_out", bufs=3))
         ctx.enter_context(tc.manual_schedule())
 
@@ -81,115 +82,121 @@ def tile_fast_tucker_taylor_pa_s_kernel(tc, z, G2_words, G2_scales, out):
                 in_=ident_bf16[:].rearrange("v (h u e j) -> v u j h e", h=2, u=2, e=2)[:, u, :, :, :],
             )
 
-        z12_psum = psum_z.tile([P, 2, P], BF16)
-        nc.tensor.transpose(z12_psum[:, 0, :], z_rows[:, 1, :], ident_bf16[:])
-        nc.tensor.transpose(z12_psum[:, 1, :], z_rows[:, 2, :], ident_bf16[:])
+        sort_flat = sort_ujhe[:].rearrange("v u y -> v (u y)")
+        z_psum = psum_z.tile([P, 3, P], BF16)
+        nc.tensor.transpose(z_psum[:, 1, :], z_rows[:, 1, :], ident_bf16[:])
+        nc.tensor.transpose(z_psum[:, 0, :], z_rows[:, 0, :], sort_flat)
+        nc.tensor.transpose(z_psum[:, 2, :], z_rows[:, 2, :], ident_bf16[:])
         acc = psum_out.tile([P, 2, P], BF16)
-        nc.tensor.transpose(acc[:, 0, :], z_rows[:, 0, :], sort_ujhe[:].rearrange("v u y -> v (u y)"))
         nc.tensor.transpose(acc[:, 1, :], z_rows[:, 2, :], ident_bf16[:])
+        nc.tensor.transpose(acc[:, 0, :], z_rows[:, 0, :], sort_flat)
         z1h = keep.tile([P, N_TILES, BH], BF16)
         nc.vector.tensor_copy(
             out=z1h[:].rearrange("x j (b h) -> x j b h", h=2),
-            in_=z12_psum[:, 0, :].rearrange("x (b j) -> x j b", b=RANK).unsqueeze(3).to_broadcast([P, N_TILES, RANK, 2]),
+            in_=z_psum[:, 1, :].rearrange("x (b j) -> x j b", b=RANK).unsqueeze(3).to_broadcast([P, N_TILES, RANK, 2]),
         )
-        z2_psum = z12_psum[:, 1, :]
-        z0_sorted = keep.tile([P, P], BF16)
-        nc.scalar.copy(out=z0_sorted[:], in_=acc[:, 0, :])
         z2_f32 = keep.tile([P, P], F32)
         nc.scalar.copy(out=z2_f32[:], in_=acc[:, 1, :])
+        z0_sorted = keep.tile([P, P], BF16)
+        nc.scalar.copy(out=z0_sorted[:], in_=acc[:, 0, :])
 
-        def z1_of(r):
-            tiles = slice(first_tiles[r], first_tiles[r] + ROUND_TILES[r])
-            return z1h[:, tiles, :].rearrange("x j (b h) -> x j b h", h=2)[:, :, :, 0]
+        def z1_of(first, n_tiles):
+            return z1h[:, first : first + n_tiles, :].rearrange("x j (b h) -> x j b h", h=2)[:, :, :, 0]
 
-        def z0_of(r, first, n_tiles, u):
-            start = u * (P // 2) + (first_tiles[r] + first) * HE
-            return z0_sorted[:, start : start + n_tiles * HE].rearrange("x (j he) -> x j he", he=HE)
+        def z2_of(first, n_tiles):
+            return z_psum[:, 2, :].rearrange("x (c j) -> x j c", c=RANK)[:, first : first + n_tiles, :]
 
-        def pair_products(r):
-            tiles = slice(first_tiles[r], first_tiles[r] + ROUND_TILES[r])
-            shape = [P, ROUND_TILES[r], RANK, BH]
-            pair_t = work.tile([P, ROUND_TILES[r], P], F32)
+        def z0_of(source, first, n_tiles, u):
+            start = u * (P // 2) + first * HE
+            return source[:, start : start + n_tiles * HE].rearrange("x (j he) -> x j he", he=HE)
+
+        def pair_products(first, n_tiles):
+            shape = [P, n_tiles, RANK, BH]
+            pair_t = work.tile([P, n_tiles, P], F32)
             nc.vector.tensor_tensor(
                 out=pair_t[:].rearrange("x j (c bh) -> x j c bh", bh=BH),
-                in0=z2_psum.rearrange("x (c j) -> x j c", c=RANK)[:, tiles, :].unsqueeze(3).to_broadcast(shape),
-                in1=z1h[:, tiles, :].unsqueeze(2).to_broadcast(shape),
+                in0=z2_of(first, n_tiles).unsqueeze(3).to_broadcast(shape),
+                in1=z1h[:, first : first + n_tiles, :].unsqueeze(2).to_broadcast(shape),
                 op=MULT,
             )
-            turned = psum_turn.tile([P, ROUND_TILES[r], P], F32)
-            for i in range(ROUND_TILES[r]):
-                nc.tensor.transpose(turned[:, i, :], pair_t[:, i, :], ident_f32[:])
-            return turned
+            return pair_t
+
+        def turn(pair_t, first, n_tiles):
+            pair = psum_pair.tile([P, n_tiles, P], F32)
+            for i in range(n_tiles):
+                nc.tensor.transpose(pair[:, i, :], pair_t[:, first + i, :], ident_f32[:])
+            return pair
 
         def last_products(pair, r):
             n = ROUND_TILES[r] * P
             grouped = work.tile([P, n * PACK], BF16, align_bytes=64)
             nc.vector.tensor_tensor(
                 out=grouped[:].rearrange("p (n t) -> p n t", t=PACK),
-                in0=pair[:].rearrange("p i x -> p (i x)").unsqueeze(2).to_broadcast([P, n, PACK]),
+                in0=pair.rearrange("p i x -> p (i x)").unsqueeze(2).to_broadcast([P, n, PACK]),
                 in1=a_reps[r][:].rearrange("p t n -> p n t"),
                 op=MULT,
             )
             return grouped
 
-        def regroup(kron_t, grouped, bank_tile):
-            grouped_words = grouped[:].bitcast(F32).rearrange("p (j x u) -> p j x u", x=P, u=2)
+        def turn_words(kron_t, bank_tile):
             turned = psum_turn.tile([P, BANK_TILES, 2, P], F32)
             for i in range(BANK_TILES):
                 for u in range(2):
                     nc.tensor.transpose(turned[:, i, u, :], kron_t[:, bank_tile + i, u, :].bitcast(F32), ident_f32[:])
-            nc.scalar.copy(
+            return turned
+
+        def empty_words(engine_copy, turned, grouped, bank_tile):
+            grouped_words = grouped[:].bitcast(F32).rearrange("p (j x u) -> p j x u", x=P, u=2)
+            engine_copy(
                 out=grouped_words[:, bank_tile : bank_tile + BANK_TILES, :, :],
                 in_=turned[:].rearrange("p i u x -> p i x u"),
             )
 
-        def multiply(grouped, r, vector_helps):
-            width = ROUND_TILES[r] * P
+        def quantise(grouped_cols, width):
             codes = work.tile([P, width], U32, align_bytes=64)
             scales = work.tile([P, width], U8, align_bytes=64)
-            nc.vector.quantize_mx(out=codes[:].bitcast(FP8X4), scales=scales[:], in_=grouped[:])
+            nc.vector.quantize_mx(out=codes[:].bitcast(FP8X4), scales=scales[:], in_=grouped_cols)
+            return codes, scales
+
+        def matmuls(quantised, width):
+            accs = []
             for half in range(OUT_ROWS // P):
                 acc = psum_out.tile([P, width], F32)
                 nc.tensor.matmul_mx(
                     out=acc[:],
                     lhsT=w_words[:, 2 * P * half : 2 * P * (half + 1)].bitcast(FP4X4),
                     lhsT_scale=w_scales[:, P * half : P * (half + 1)],
-                    rhs=codes[:].bitcast(FP8X4),
-                    rhs_scale=scales[:],
+                    rhs=quantised[0][:].bitcast(FP8X4),
+                    rhs_scale=quantised[1][:],
                     start=True,
                     stop=True,
                 )
-                result = stage.tile([P, width], F32)
-                if vector_helps and half == 1:
-                    nc.vector.tensor_copy(out=result[:], in_=acc[:])
-                else:
-                    nc.scalar.copy(out=result[:], in_=acc[:])
-                nc.sync.dma_start(
-                    out=out[P * half : P * (half + 1), first_tiles[r] * P : first_tiles[r] * P + width], in_=result[:]
-                )
+                accs.append(acc)
+            return accs
+
+        def store(engine_copy, acc, half, first, width):
+            result = stage.tile([P, width], F32)
+            engine_copy(out=result[:], in_=acc[:])
+            nc.sync.dma_start(out=out[P * half : P * (half + 1), first * P : first * P + width], in_=result[:])
 
         S, G = SCALAR_ROUND, GPSIMD_ROUND
         n_s, n_g = ROUND_TILES[S], ROUND_TILES[G]
-        pairs = {}
-        groupeds = {}
-        pairs[0] = pair_products(0)
-        pairs[1] = pair_products(1)
-        pairs[4] = pair_products(4)
+        f_s, f_g = first_tiles[S], first_tiles[G]
+        V_COPY, S_COPY = nc.vector.tensor_copy, nc.scalar.copy
 
         ba_t = keep.tile([P, n_s, 2, RANK * HE], F32)
         for u in range(2):
-            nc.gpsimd.tensor_tensor(
+            nc.vector.tensor_tensor(
                 out=ba_t[:, :, u, :].rearrange("x j (b he) -> x j b he", he=HE),
-                in0=z1_of(S).unsqueeze(3).to_broadcast([P, n_s, RANK, HE]),
-                in1=z0_of(S, 0, n_s, u).unsqueeze(2).to_broadcast([P, n_s, RANK, HE]),
+                in0=z1_of(f_s, n_s).unsqueeze(3).to_broadcast([P, n_s, RANK, HE]),
+                in1=z0_of(z_psum[:, 0, :], f_s, n_s, u).unsqueeze(2).to_broadcast([P, n_s, RANK, HE]),
                 op=MULT,
             )
         bc_t = keep.tile([P, n_g, RANK * RANK], F32)
-        g_tiles = slice(first_tiles[G], first_tiles[G] + n_g)
-        nc.gpsimd.tensor_tensor(
+        nc.vector.tensor_tensor(
             out=bc_t[:].rearrange("x j (c b) -> x j c b", b=RANK),
-            in0=z2_f32[:].rearrange("x (c j) -> x j c", c=RANK)[:, g_tiles, :].unsqueeze(3).to_broadcast([P, n_g, RANK, RANK]),
-            in1=z1_of(G).unsqueeze(2).to_broadcast([P, n_g, RANK, RANK]),
+            in0=z2_of(f_g, n_g).unsqueeze(3).to_broadcast([P, n_g, RANK, RANK]),
+            in1=z1_of(f_g, n_g).unsqueeze(2).to_broadcast([P, n_g, RANK, RANK]),
             op=MULT,
         )
 
@@ -199,7 +206,7 @@ def tile_fast_tucker_taylor_pa_s_kernel(tc, z, G2_words, G2_scales, out):
         def scalar_products(bank_tile):
             for i in range(bank_tile, bank_tile + BANK_TILES):
                 for c in range(RANK):
-                    col = c * N_TILES + first_tiles[S] + i
+                    col = c * N_TILES + f_s + i
                     nc.scalar.activation(
                         out=kron_t_s[:, i, :, RANK * HE * c : RANK * HE * (c + 1)],
                         in_=ba_t[:, i, :, :],
@@ -207,32 +214,54 @@ def tile_fast_tucker_taylor_pa_s_kernel(tc, z, G2_words, G2_scales, out):
                         scale=z2_f32[:, col : col + 1],
                     )
 
-        def gpsimd_products(bank_tile):
+        def gpsimd_products(first, n_tiles):
             for u in range(2):
                 nc.gpsimd.tensor_tensor(
-                    out=kron_t_g[:, bank_tile : bank_tile + BANK_TILES, u, :].rearrange("x j (cb he) -> x j cb he", he=HE),
-                    in0=bc_t[:, bank_tile : bank_tile + BANK_TILES, :].unsqueeze(3).to_broadcast([P, BANK_TILES, RANK * RANK, HE]),
-                    in1=z0_of(G, bank_tile, BANK_TILES, u).unsqueeze(2).to_broadcast([P, BANK_TILES, RANK * RANK, HE]),
+                    out=kron_t_g[:, first : first + n_tiles, u, :].rearrange("x j (cb he) -> x j cb he", he=HE),
+                    in0=bc_t[:, first : first + n_tiles, :].unsqueeze(3).to_broadcast([P, n_tiles, RANK * RANK, HE]),
+                    in1=z0_of(z0_sorted, f_g + first, n_tiles, u).unsqueeze(2).to_broadcast([P, n_tiles, RANK * RANK, HE]),
                     op=MULT,
                 )
 
         grouped_s = work.tile([P, n_s * P * PACK], BF16, align_bytes=64, tag="grouped")
         grouped_g = work.tile([P, n_g * P * PACK], BF16, align_bytes=64, tag="grouped")
-        groupeds[S] = grouped_s
-        groupeds[G] = grouped_g
-        gpsimd_products(0)
-        gpsimd_products(BANK_TILES)
+        for i in range(n_g):
+            gpsimd_products(i, 1)
         scalar_products(0)
         scalar_products(BANK_TILES)
-        groupeds[0] = last_products(pairs[0], 0)
-        regroup(kron_t_s, grouped_s, 0)
-        regroup(kron_t_s, grouped_s, BANK_TILES)
-        groupeds[1] = last_products(pairs[1], 1)
-        groupeds[4] = last_products(pairs[4], 4)
-        multiply(groupeds[0], 0, False)
-        regroup(kron_t_g, grouped_g, 0)
-        multiply(groupeds[1], 1, False)
-        regroup(kron_t_g, grouped_g, BANK_TILES)
-        multiply(groupeds[2], 2, True)
-        multiply(groupeds[3], 3, True)
-        multiply(groupeds[4], 4, True)
+        pair_t01 = pair_products(0, 6)
+        pair_t4 = pair_products(14, 2)
+        pair0 = turn(pair_t01, 0, 2)
+        pair1 = turn(pair_t01, 2, 4)
+        words_s0 = turn_words(kron_t_s, 0)
+        words_s1 = turn_words(kron_t_s, BANK_TILES)
+        grouped0 = last_products(pair0[:], 0)
+        pair4 = turn(pair_t4, 0, 2)
+        empty_words(S_COPY, words_s0, grouped_s, 0)
+        empty_words(S_COPY, words_s1, grouped_s, BANK_TILES)
+        words_g0 = turn_words(kron_t_g, 0)
+        words_g1 = turn_words(kron_t_g, BANK_TILES)
+        empty_words(S_COPY, words_g0, grouped_g, 0)
+        empty_words(S_COPY, words_g1, grouped_g, BANK_TILES)
+        grouped1 = last_products(pair1[:], 1)
+        q0 = quantise(grouped0[:], 256)
+        acc0 = matmuls(q0, 256)
+        store(S_COPY, acc0[0], 0, 0, 256)
+        store(S_COPY, acc0[1], 1, 0, 256)
+        qs = quantise(grouped_s[:], 512)
+        accs = matmuls(qs, 512)
+        store(S_COPY, accs[0], 0, f_s, 512)
+        store(S_COPY, accs[1], 1, f_s, 512)
+        q1 = quantise(grouped1[:], 512)
+        acc1 = matmuls(q1, 512)
+        store(S_COPY, acc1[0], 0, 2, 512)
+        store(S_COPY, acc1[1], 1, 2, 512)
+        grouped4 = last_products(pair4[:], 4)
+        qg = quantise(grouped_g[:], 512)
+        accg = matmuls(qg, 512)
+        q4 = quantise(grouped4[:], 256)
+        store(S_COPY, accg[0], 0, f_g, 512)
+        store(V_COPY, accg[1], 1, f_g, 512)
+        acc4 = matmuls(q4, 256)
+        store(S_COPY, acc4[0], 0, 14, 256)
+        store(V_COPY, acc4[1], 1, 14, 256)

@@ -24,8 +24,6 @@ N_TILES = SAMPLES // P
 OUT_ROWS = 256
 BANK_TILES = 2
 ROUND_TILES = (2, 4, 4, 4, 2)
-SCALAR_ROUND = 2
-GPSIMD_ROUND = 3
 
 FLOPS = 2 * OUT_ROWS * K * SAMPLES
 
@@ -37,6 +35,7 @@ def tile_fast_tucker_taylor_pa_s_kernel(tc, z, G2_words, G2_scales, out):
     with ExitStack() as ctx:
         keep = ctx.enter_context(tc.tile_pool(name="keep", bufs=1))
         work = ctx.enter_context(tc.tile_pool(name="work", bufs=n_rounds))
+        big = ctx.enter_context(tc.tile_pool(name="big", bufs=6))
         stage = ctx.enter_context(tc.tile_pool(name="stage", bufs=4))
         psum_z = ctx.enter_context(tc.psum_pool(name="psum_z", bufs=1))
         psum_pair = ctx.enter_context(tc.psum_pool(name="psum_pair", bufs=2))
@@ -62,7 +61,7 @@ def tile_fast_tucker_taylor_pa_s_kernel(tc, z, G2_words, G2_scales, out):
         a_reps[1] = load_a_rep(1)
         w_words = keep.tile([P, 2 * OUT_ROWS], U8, align_bytes=64)
         nc.sync.dma_start(out=w_words[:].bitcast(I32), in_=G2_words[0].bitcast(I32))
-        a_reps[4] = load_a_rep(4)
+        a_reps[3] = load_a_rep(3)
         w_scales = keep.tile([P, OUT_ROWS], U8, align_bytes=64)
         nc.vector.memset(w_scales[:].bitcast(I32), 0)
         for quad in range(4):
@@ -103,19 +102,22 @@ def tile_fast_tucker_taylor_pa_s_kernel(tc, z, G2_words, G2_scales, out):
         def z1_of(first, n_tiles):
             return z1h[:, first : first + n_tiles, :].rearrange("x j (b h) -> x j b h", h=2)[:, :, :, 0]
 
-        def z2_of(first, n_tiles):
-            return z_psum[:, 2, :].rearrange("x (c j) -> x j c", c=RANK)[:, first : first + n_tiles, :]
+        engines = {"vector": nc.vector, "gpsimd": nc.gpsimd}
+        z2_sources = {"vector": z_psum[:, 2, :], "gpsimd": z2_f32[:]}
+
+        def z2_of(who, first, n_tiles):
+            return z2_sources[who].rearrange("x (c j) -> x j c", c=RANK)[:, first : first + n_tiles, :]
 
         def z0_of(source, first, n_tiles, u):
             start = u * (P // 2) + first * HE
             return source[:, start : start + n_tiles * HE].rearrange("x (j he) -> x j he", he=HE)
 
-        def pair_products(first, n_tiles):
+        def pair_products(who, first, n_tiles):
             shape = [P, n_tiles, RANK, BH]
             pair_t = work.tile([P, n_tiles, P], F32)
-            nc.vector.tensor_tensor(
+            engines[who].tensor_tensor(
                 out=pair_t[:].rearrange("x j (c bh) -> x j c bh", bh=BH),
-                in0=z2_of(first, n_tiles).unsqueeze(3).to_broadcast(shape),
+                in0=z2_of(who, first, n_tiles).unsqueeze(3).to_broadcast(shape),
                 in1=z1h[:, first : first + n_tiles, :].unsqueeze(2).to_broadcast(shape),
                 op=MULT,
             )
@@ -127,13 +129,13 @@ def tile_fast_tucker_taylor_pa_s_kernel(tc, z, G2_words, G2_scales, out):
                 nc.tensor.transpose(pair[:, i, :], pair_t[:, first + i, :], ident_f32[:])
             return pair
 
-        def last_products(pair, r):
-            n = ROUND_TILES[r] * P
-            grouped = work.tile([P, n * PACK], BF16, align_bytes=64)
+        def last_products(pair, r, first=0, n_tiles=None):
+            n = (n_tiles or ROUND_TILES[r]) * P
+            grouped = big.tile([P, n * PACK], BF16, align_bytes=64)
             nc.vector.tensor_tensor(
                 out=grouped[:].rearrange("p (n t) -> p n t", t=PACK),
                 in0=pair.rearrange("p i x -> p (i x)").unsqueeze(2).to_broadcast([P, n, PACK]),
-                in1=a_reps[r][:].rearrange("p t n -> p n t"),
+                in1=a_reps[r][:, :, first * P : first * P + n].rearrange("p t n -> p n t"),
                 op=MULT,
             )
             return grouped
@@ -153,8 +155,8 @@ def tile_fast_tucker_taylor_pa_s_kernel(tc, z, G2_words, G2_scales, out):
             )
 
         def quantise(grouped_cols, width):
-            codes = work.tile([P, width], U32, align_bytes=64)
-            scales = work.tile([P, width], U8, align_bytes=64)
+            codes = big.tile([P, width], U32, align_bytes=64)
+            scales = big.tile([P, width], U8, align_bytes=64)
             nc.vector.quantize_mx(out=codes[:].bitcast(FP8X4), scales=scales[:], in_=grouped_cols)
             return codes, scales
 
@@ -174,94 +176,115 @@ def tile_fast_tucker_taylor_pa_s_kernel(tc, z, G2_words, G2_scales, out):
                 accs.append(acc)
             return accs
 
+        def matmuls_one_bank(quantised, width):
+            acc = psum_out.tile([P, OUT_ROWS // P, width], F32)
+            for half in range(OUT_ROWS // P):
+                nc.tensor.matmul_mx(
+                    out=acc[:, half, :],
+                    lhsT=w_words[:, 2 * P * half : 2 * P * (half + 1)].bitcast(FP4X4),
+                    lhsT_scale=w_scales[:, P * half : P * (half + 1)],
+                    rhs=quantised[0][:].bitcast(FP8X4),
+                    rhs_scale=quantised[1][:],
+                    start=True,
+                    stop=True,
+                )
+            return acc
+
+        def store_both(engine_copy, acc, first, width):
+            result = stage.tile([P, OUT_ROWS // P, width], F32)
+            engine_copy(out=result[:], in_=acc[:])
+            nc.sync.dma_start(out=out.rearrange("(half p) n -> p half n", p=P)[:, :, first * P : first * P + width], in_=result[:])
+
         def store(engine_copy, acc, half, first, width):
             result = stage.tile([P, width], F32)
             engine_copy(out=result[:], in_=acc[:])
             nc.sync.dma_start(out=out[P * half : P * (half + 1), first * P : first * P + width], in_=result[:])
 
-        S, G = SCALAR_ROUND, GPSIMD_ROUND
-        n_s, n_g = ROUND_TILES[S], ROUND_TILES[G]
-        f_s, f_g = first_tiles[S], first_tiles[G]
+        f_s, f_v, f_g = 6, 8, 14
         V_COPY, S_COPY = nc.vector.tensor_copy, nc.scalar.copy
 
-        ba_t = keep.tile([P, n_s, 2, RANK * HE], F32)
+        ba_t = keep.tile([P, 2, 2, RANK * HE], F32)
         for u in range(2):
             nc.vector.tensor_tensor(
                 out=ba_t[:, :, u, :].rearrange("x j (b he) -> x j b he", he=HE),
-                in0=z1_of(f_s, n_s).unsqueeze(3).to_broadcast([P, n_s, RANK, HE]),
-                in1=z0_of(z_psum[:, 0, :], f_s, n_s, u).unsqueeze(2).to_broadcast([P, n_s, RANK, HE]),
+                in0=z1_of(f_s, 2).unsqueeze(3).to_broadcast([P, 2, RANK, HE]),
+                in1=z0_of(z_psum[:, 0, :], f_s, 2, u).unsqueeze(2).to_broadcast([P, 2, RANK, HE]),
                 op=MULT,
             )
-        bc_t = keep.tile([P, n_g, RANK * RANK], F32)
-        nc.vector.tensor_tensor(
-            out=bc_t[:].rearrange("x j (c b) -> x j c b", b=RANK),
-            in0=z2_of(f_g, n_g).unsqueeze(3).to_broadcast([P, n_g, RANK, RANK]),
-            in1=z1_of(f_g, n_g).unsqueeze(2).to_broadcast([P, n_g, RANK, RANK]),
-            op=MULT,
-        )
+        kron_t = keep.tile([P, 6, 2, K // 2], BF16)
 
-        kron_t_s = keep.tile([P, n_s, 2, K // 2], BF16)
-        kron_t_g = keep.tile([P, n_g, 2, K // 2], BF16)
+        def bc_products(who, first):
+            bc_t = work.tile([P, 2, RANK * RANK], F32)
+            engines[who].tensor_tensor(
+                out=bc_t[:].rearrange("x j (c b) -> x j c b", b=RANK),
+                in0=z2_of(who, first, 2).unsqueeze(3).to_broadcast([P, 2, RANK, RANK]),
+                in1=z1_of(first, 2).unsqueeze(2).to_broadcast([P, 2, RANK, RANK]),
+                op=MULT,
+            )
+            return bc_t
 
-        def scalar_products(bank_tile):
-            for i in range(bank_tile, bank_tile + BANK_TILES):
+        def scalar_products():
+            for i in range(2):
                 for c in range(RANK):
                     col = c * N_TILES + f_s + i
                     nc.scalar.activation(
-                        out=kron_t_s[:, i, :, RANK * HE * c : RANK * HE * (c + 1)],
+                        out=kron_t[:, i, :, RANK * HE * c : RANK * HE * (c + 1)],
                         in_=ba_t[:, i, :, :],
                         func=COPY,
                         scale=z2_f32[:, col : col + 1],
                     )
 
-        def gpsimd_products(first, n_tiles):
+        def sample_products(engine, z0_source, bc_t, slot, first, i, n):
             for u in range(2):
-                nc.gpsimd.tensor_tensor(
-                    out=kron_t_g[:, first : first + n_tiles, u, :].rearrange("x j (cb he) -> x j cb he", he=HE),
-                    in0=bc_t[:, first : first + n_tiles, :].unsqueeze(3).to_broadcast([P, n_tiles, RANK * RANK, HE]),
-                    in1=z0_of(z0_sorted, f_g + first, n_tiles, u).unsqueeze(2).to_broadcast([P, n_tiles, RANK * RANK, HE]),
+                engine.tensor_tensor(
+                    out=kron_t[:, slot + i : slot + i + n, u, :].rearrange("x j (cb he) -> x j cb he", he=HE),
+                    in0=bc_t[:, i : i + n, :].unsqueeze(3).to_broadcast([P, n, RANK * RANK, HE]),
+                    in1=z0_of(z0_source, first + i, n, u).unsqueeze(2).to_broadcast([P, n, RANK * RANK, HE]),
                     op=MULT,
                 )
 
-        grouped_s = work.tile([P, n_s * P * PACK], BF16, align_bytes=64, tag="grouped")
-        grouped_g = work.tile([P, n_g * P * PACK], BF16, align_bytes=64, tag="grouped")
-        for i in range(n_g):
-            gpsimd_products(i, 1)
-        scalar_products(0)
-        scalar_products(BANK_TILES)
-        pair_t01 = pair_products(0, 6)
-        pair_t4 = pair_products(14, 2)
-        pair0 = turn(pair_t01, 0, 2)
-        pair1 = turn(pair_t01, 2, 4)
-        words_s0 = turn_words(kron_t_s, 0)
-        words_s1 = turn_words(kron_t_s, BANK_TILES)
+        grouped_x = big.tile([P, 4 * P * PACK], BF16, align_bytes=64, tag="grouped")
+        grouped_g = big.tile([P, 2 * P * PACK], BF16, align_bytes=64, tag="grouped")
+        scalar_products()
+        pair_t0 = pair_products("vector", 0, 2)
+        pair0 = turn(pair_t0, 0, 2)
+        bc_v = bc_products("vector", f_v)
+        sample_products(nc.vector, z_psum[:, 0, :], bc_v, 2, f_v, 0, 2)
+        pair_t1 = pair_products("gpsimd", 2, 4)
+        pair_t2 = pair_products("gpsimd", 10, 4)
+        bc_g = bc_products("gpsimd", f_g)
+        sample_products(nc.gpsimd, z0_sorted, bc_g, 4, f_g, 0, 1)
+        sample_products(nc.gpsimd, z0_sorted, bc_g, 4, f_g, 1, 1)
+        pair1 = turn(pair_t1, 0, 4)
+        words_v = turn_words(kron_t, 2)
+        words_s = turn_words(kron_t, 0)
+        empty_words(S_COPY, words_s, grouped_x, 0)
+        empty_words(S_COPY, words_v, grouped_x, 2)
         grouped0 = last_products(pair0[:], 0)
-        pair4 = turn(pair_t4, 0, 2)
-        empty_words(S_COPY, words_s0, grouped_s, 0)
-        empty_words(S_COPY, words_s1, grouped_s, BANK_TILES)
-        words_g0 = turn_words(kron_t_g, 0)
-        words_g1 = turn_words(kron_t_g, BANK_TILES)
-        empty_words(S_COPY, words_g0, grouped_g, 0)
-        empty_words(S_COPY, words_g1, grouped_g, BANK_TILES)
+        pair2 = turn(pair_t2, 0, 4)
         grouped1 = last_products(pair1[:], 1)
         q0 = quantise(grouped0[:], 256)
-        acc0 = matmuls(q0, 256)
-        store(S_COPY, acc0[0], 0, 0, 256)
-        store(S_COPY, acc0[1], 1, 0, 256)
-        qs = quantise(grouped_s[:], 512)
-        accs = matmuls(qs, 512)
-        store(S_COPY, accs[0], 0, f_s, 512)
-        store(S_COPY, accs[1], 1, f_s, 512)
+        acc0 = matmuls_one_bank(q0, 256)
+        store_both(S_COPY, acc0, 0, 256)
+        qx = quantise(grouped_x[:], 512)
+        accx = matmuls(qx, 512)
+        store(S_COPY, accx[0], 0, f_s, 512)
+        store(S_COPY, accx[1], 1, f_s, 512)
         q1 = quantise(grouped1[:], 512)
+        words_g = turn_words(kron_t, 4)
+        empty_words(S_COPY, words_g, grouped_g, 0)
         acc1 = matmuls(q1, 512)
         store(S_COPY, acc1[0], 0, 2, 512)
         store(S_COPY, acc1[1], 1, 2, 512)
-        grouped4 = last_products(pair4[:], 4)
-        qg = quantise(grouped_g[:], 512)
-        accg = matmuls(qg, 512)
-        q4 = quantise(grouped4[:], 256)
-        store(S_COPY, accg[0], 0, f_g, 512)
-        store(V_COPY, accg[1], 1, f_g, 512)
-        acc4 = matmuls(q4, 256)
-        store(S_COPY, acc4[0], 0, 14, 256)
-        store(V_COPY, acc4[1], 1, 14, 256)
+        grouped2a = last_products(pair2[:, 0:2, :], 3, 0, 2)
+        grouped2b = last_products(pair2[:, 2:4, :], 3, 2, 2)
+        qg = quantise(grouped_g[:], 256)
+        accg = matmuls_one_bank(qg, 256)
+        store_both(S_COPY, accg, f_g, 256)
+        q2a = quantise(grouped2a[:], 256)
+        acc2a = matmuls_one_bank(q2a, 256)
+        q2b = quantise(grouped2b[:], 256)
+        store_both(V_COPY, acc2a, 10, 256)
+        acc2b = matmuls(q2b, 256)
+        store(S_COPY, acc2b[0], 0, 12, 256)
+        store(V_COPY, acc2b[1], 1, 12, 256)

@@ -36,7 +36,7 @@ def tile_fast_tucker_taylor_pa_s_kernel(tc, z, G2_words, G2_scales, out):
         keep = ctx.enter_context(tc.tile_pool(name="keep", bufs=1))
         work = ctx.enter_context(tc.tile_pool(name="work", bufs=n_rounds))
         big = ctx.enter_context(tc.tile_pool(name="big", bufs=6))
-        stage = ctx.enter_context(tc.tile_pool(name="stage", bufs=4))
+        stage = ctx.enter_context(tc.tile_pool(name="stage", bufs=10))
         psum_z = ctx.enter_context(tc.psum_pool(name="psum_z", bufs=1))
         psum_pair = ctx.enter_context(tc.psum_pool(name="psum_pair", bufs=2))
         psum_turn = ctx.enter_context(tc.psum_pool(name="psum_turn", bufs=2))

@@ -200,31 +200,32 @@ def tile_fast_tucker_taylor_pa_s_kernel(tc, z, G2_words, G2_scales, out):
             engine_copy(out=result[:], in_=acc[:])
             nc.sync.dma_start(out=out[P * half : P * (half + 1), first * P : first * P + width], in_=result[:])
 
-        f_s, f_v, f_g = 6, 8, 14
+        f_s, f_v, f_g = 6, 9, 14
+        n_s = 3
         V_COPY, S_COPY = nc.vector.tensor_copy, nc.scalar.copy
 
-        ba_t = keep.tile([P, 2, 2, RANK * HE], F32)
+        ba_t = keep.tile([P, n_s, 2, RANK * HE], F32)
         for u in range(2):
             nc.vector.tensor_tensor(
                 out=ba_t[:, :, u, :].rearrange("x j (b he) -> x j b he", he=HE),
-                in0=z1_of(f_s, 2).unsqueeze(3).to_broadcast([P, 2, RANK, HE]),
-                in1=z0_of(z_psum[:, 0, :], f_s, 2, u).unsqueeze(2).to_broadcast([P, 2, RANK, HE]),
+                in0=z1_of(f_s, n_s).unsqueeze(3).to_broadcast([P, n_s, RANK, HE]),
+                in1=z0_of(z_psum[:, 0, :], f_s, n_s, u).unsqueeze(2).to_broadcast([P, n_s, RANK, HE]),
                 op=MULT,
             )
         kron_t = keep.tile([P, 6, 2, K // 2], BF16)
 
-        def bc_products(who, first):
-            bc_t = work.tile([P, 2, RANK * RANK], F32)
+        def bc_products(who, first, n=2):
+            bc_t = work.tile([P, n, RANK * RANK], F32)
             engines[who].tensor_tensor(
                 out=bc_t[:].rearrange("x j (c b) -> x j c b", b=RANK),
-                in0=z2_of(who, first, 2).unsqueeze(3).to_broadcast([P, 2, RANK, RANK]),
-                in1=z1_of(first, 2).unsqueeze(2).to_broadcast([P, 2, RANK, RANK]),
+                in0=z2_of(who, first, n).unsqueeze(3).to_broadcast([P, n, RANK, RANK]),
+                in1=z1_of(first, n).unsqueeze(2).to_broadcast([P, n, RANK, RANK]),
                 op=MULT,
             )
             return bc_t
 
         def scalar_products():
-            for i in range(2):
+            for i in range(n_s):
                 for c in range(RANK):
                     col = c * N_TILES + f_s + i
                     nc.scalar.activation(
@@ -248,16 +249,16 @@ def tile_fast_tucker_taylor_pa_s_kernel(tc, z, G2_words, G2_scales, out):
         scalar_products()
         pair_t0 = pair_products("vector", 0, 2)
         pair0 = turn(pair_t0, 0, 2)
-        bc_v = bc_products("vector", f_v)
-        sample_products(nc.vector, z_psum[:, 0, :], bc_v, 2, f_v, 0, 2)
+        bc_v = bc_products("vector", f_v, 1)
+        sample_products(nc.vector, z_psum[:, 0, :], bc_v, 3, f_v, 0, 1)
         pair_t1 = pair_products("gpsimd", 2, 4)
         pair_t2 = pair_products("gpsimd", 10, 4)
         bc_g = bc_products("gpsimd", f_g)
         sample_products(nc.gpsimd, z0_sorted, bc_g, 4, f_g, 0, 1)
         sample_products(nc.gpsimd, z0_sorted, bc_g, 4, f_g, 1, 1)
         pair1 = turn(pair_t1, 0, 4)
-        words_v = turn_words(kron_t, 2)
         words_s = turn_words(kron_t, 0)
+        words_v = turn_words(kron_t, 2)
         empty_words(S_COPY, words_s, grouped_x, 0)
         empty_words(S_COPY, words_v, grouped_x, 2)
         grouped0 = last_products(pair0[:], 0)

@@ -37,10 +37,7 @@ def tile_fast_tucker_taylor_pa_s_kernel(tc, z, G2_words, G2_scales, out):
         work = ctx.enter_context(tc.tile_pool(name="work", bufs=n_rounds))
         big = ctx.enter_context(tc.tile_pool(name="big", bufs=6))
         stage = ctx.enter_context(tc.tile_pool(name="stage", bufs=10))
-        psum_z = ctx.enter_context(tc.psum_pool(name="psum_z", bufs=1))
-        psum_pair = ctx.enter_context(tc.psum_pool(name="psum_pair", bufs=2))
-        psum_turn = ctx.enter_context(tc.psum_pool(name="psum_turn", bufs=2))
-        psum_out = ctx.enter_context(tc.psum_pool(name="psum_out", bufs=3))
+        psum = ctx.enter_context(tc.psum_pool(name="psum", bufs=8))
         ctx.enter_context(tc.manual_schedule())
 
         z_rows = keep.tile([P, 3, P], BF16)
@@ -82,28 +79,29 @@ def tile_fast_tucker_taylor_pa_s_kernel(tc, z, G2_words, G2_scales, out):
             )
 
         sort_flat = sort_ujhe[:].rearrange("v u y -> v (u y)")
-        z_psum = psum_z.tile([P, 3, P], BF16)
-        nc.tensor.transpose(z_psum[:, 1, :], z_rows[:, 1, :], ident_bf16[:])
+        z1_psum = psum.tile([P, P], BF16, tag="bank")
+        nc.tensor.transpose(z1_psum[:], z_rows[:, 1, :], ident_bf16[:])
+        z_scalar = psum.tile([P, 2, P], BF16, tag="bank")
+        nc.tensor.transpose(z_scalar[:, 1, :], z_rows[:, 2, :], ident_bf16[:])
+        nc.tensor.transpose(z_scalar[:, 0, :], z_rows[:, 0, :], sort_flat)
+        z_psum = psum.tile([P, 2, P], BF16, tag="bank")
+        nc.tensor.transpose(z_psum[:, 1, :], z_rows[:, 2, :], ident_bf16[:])
         nc.tensor.transpose(z_psum[:, 0, :], z_rows[:, 0, :], sort_flat)
-        nc.tensor.transpose(z_psum[:, 2, :], z_rows[:, 2, :], ident_bf16[:])
-        acc = psum_out.tile([P, 2, P], BF16)
-        nc.tensor.transpose(acc[:, 1, :], z_rows[:, 2, :], ident_bf16[:])
-        nc.tensor.transpose(acc[:, 0, :], z_rows[:, 0, :], sort_flat)
         z1h = keep.tile([P, N_TILES, BH], BF16)
         nc.vector.tensor_copy(
             out=z1h[:].rearrange("x j (b h) -> x j b h", h=2),
-            in_=z_psum[:, 1, :].rearrange("x (b j) -> x j b", b=RANK).unsqueeze(3).to_broadcast([P, N_TILES, RANK, 2]),
+            in_=z1_psum[:].rearrange("x (b j) -> x j b", b=RANK).unsqueeze(3).to_broadcast([P, N_TILES, RANK, 2]),
         )
         z2_f32 = keep.tile([P, P], F32)
-        nc.scalar.copy(out=z2_f32[:], in_=acc[:, 1, :])
+        nc.scalar.copy(out=z2_f32[:], in_=z_scalar[:, 1, :])
         z0_sorted = keep.tile([P, P], BF16)
-        nc.scalar.copy(out=z0_sorted[:], in_=acc[:, 0, :])
+        nc.scalar.copy(out=z0_sorted[:], in_=z_scalar[:, 0, :])
 
         def z1_of(first, n_tiles):
             return z1h[:, first : first + n_tiles, :].rearrange("x j (b h) -> x j b h", h=2)[:, :, :, 0]
 
         engines = {"vector": nc.vector, "gpsimd": nc.gpsimd}
-        z2_sources = {"vector": z_psum[:, 2, :], "gpsimd": z2_f32[:]}
+        z2_sources = {"vector": z_psum[:, 1, :], "gpsimd": z2_f32[:]}
 
         def z2_of(who, first, n_tiles):
             return z2_sources[who].rearrange("x (c j) -> x j c", c=RANK)[:, first : first + n_tiles, :]
@@ -124,7 +122,7 @@ def tile_fast_tucker_taylor_pa_s_kernel(tc, z, G2_words, G2_scales, out):
             return pair_t
 
         def turn(pair_t, first, n_tiles):
-            pair = psum_pair.tile([P, n_tiles, P], F32)
+            pair = psum.tile([P, n_tiles, P], F32, tag="bank")
             for i in range(n_tiles):
                 nc.tensor.transpose(pair[:, i, :], pair_t[:, first + i, :], ident_f32[:])
             return pair
@@ -141,7 +139,7 @@ def tile_fast_tucker_taylor_pa_s_kernel(tc, z, G2_words, G2_scales, out):
             return grouped
 
         def turn_words(kron_t, bank_tile):
-            turned = psum_turn.tile([P, BANK_TILES, 2, P], F32)
+            turned = psum.tile([P, BANK_TILES, 2, P], F32, tag="bank")
             for i in range(BANK_TILES):
                 for u in range(2):
                     nc.tensor.transpose(turned[:, i, u, :], kron_t[:, bank_tile + i, u, :].bitcast(F32), ident_f32[:])
@@ -163,7 +161,7 @@ def tile_fast_tucker_taylor_pa_s_kernel(tc, z, G2_words, G2_scales, out):
         def matmuls(quantised, width):
             accs = []
             for half in range(OUT_ROWS // P):
-                acc = psum_out.tile([P, width], F32)
+                acc = psum.tile([P, width], F32, tag="bank")
                 nc.tensor.matmul_mx(
                     out=acc[:],
                     lhsT=w_words[:, 2 * P * half : 2 * P * (half + 1)].bitcast(FP4X4),
@@ -177,7 +175,7 @@ def tile_fast_tucker_taylor_pa_s_kernel(tc, z, G2_words, G2_scales, out):
             return accs
 
         def matmuls_one_bank(quantised, width):
-            acc = psum_out.tile([P, OUT_ROWS // P, width], F32)
+            acc = psum.tile([P, OUT_ROWS // P, width], F32, tag="bank")
             for half in range(OUT_ROWS // P):
                 nc.tensor.matmul_mx(
                     out=acc[:, half, :],

@@ -23,29 +23,27 @@ SAMPLES = 2048
 N_TILES = SAMPLES // P
 OUT_ROWS = 256
 BANK_TILES = 2
-ROUND_TILES = (2, 4, 4, 4, 2)
+LOADS = ((0, 2), (2, 4), (10, 4))
 
 FLOPS = 2 * OUT_ROWS * K * SAMPLES
 
 
 def tile_fast_tucker_taylor_pa_s_kernel(tc, z, G2_words, G2_scales, out):
     nc = tc.nc
-    n_rounds = len(ROUND_TILES)
-    first_tiles = [sum(ROUND_TILES[:r]) for r in range(n_rounds)]
     with ExitStack() as ctx:
         keep = ctx.enter_context(tc.tile_pool(name="keep", bufs=1))
-        work = ctx.enter_context(tc.tile_pool(name="work", bufs=n_rounds))
-        big = ctx.enter_context(tc.tile_pool(name="big", bufs=6))
-        stage = ctx.enter_context(tc.tile_pool(name="stage", bufs=10))
+        work = ctx.enter_context(tc.tile_pool(name="work", bufs=8))
+        big = ctx.enter_context(tc.tile_pool(name="big", bufs=8))
+        stage = ctx.enter_context(tc.tile_pool(name="stage", bufs=16))
         psum = ctx.enter_context(tc.psum_pool(name="psum", bufs=8))
         ctx.enter_context(tc.manual_schedule())
 
         z_rows = keep.tile([P, 3, P], BF16)
         nc.sync.dma_start(out=z_rows[:], in_=z.rearrange("g a (j x) -> (a j) g x", x=P))
 
-        def load_a_rep(r):
-            width = ROUND_TILES[r] * P
-            cols = slice(first_tiles[r] * P, first_tiles[r] * P + width)
+        def load_a_rep(first, n_tiles):
+            width = n_tiles * P
+            cols = slice(first * P, first * P + width)
             a_rep = work.tile([P, PACK, width], BF16)
             for h in range(2):
                 nc.sync.dma_start(
@@ -54,11 +52,12 @@ def tile_fast_tucker_taylor_pa_s_kernel(tc, z, G2_words, G2_scales, out):
             return a_rep
 
         a_reps = {}
-        a_reps[0] = load_a_rep(0)
-        a_reps[1] = load_a_rep(1)
+        for first, n_tiles in LOADS[:2]:
+            a_reps[first, n_tiles] = load_a_rep(first, n_tiles)
         w_words = keep.tile([P, 2 * OUT_ROWS], U8, align_bytes=64)
         nc.sync.dma_start(out=w_words[:].bitcast(I32), in_=G2_words[0].bitcast(I32))
-        a_reps[3] = load_a_rep(3)
+        for first, n_tiles in LOADS[2:]:
+            a_reps[first, n_tiles] = load_a_rep(first, n_tiles)
         w_scales = keep.tile([P, OUT_ROWS], U8, align_bytes=64)
         nc.vector.memset(w_scales[:].bitcast(I32), 0)
         for quad in range(4):
@@ -121,28 +120,32 @@ def tile_fast_tucker_taylor_pa_s_kernel(tc, z, G2_words, G2_scales, out):
             )
             return pair_t
 
+        def next_a(first, n_tiles):
+            for start, tiles in LOADS:
+                if start <= first and first + n_tiles <= start + tiles:
+                    return a_reps[start, tiles], (first - start) * P
+
         def turn(pair_t, first, n_tiles):
             pair = psum.tile([P, n_tiles, P], F32, tag="bank")
             for i in range(n_tiles):
                 nc.tensor.transpose(pair[:, i, :], pair_t[:, first + i, :], ident_f32[:])
             return pair
 
-        def last_products(pair, r, first=0, n_tiles=None):
-            n = (n_tiles or ROUND_TILES[r]) * P
-            grouped = big.tile([P, n * PACK], BF16, align_bytes=64)
+        def last_products(pair, first, n_tiles, grouped, slot):
+            n = n_tiles * P
+            a_rep, col = next_a(first, n_tiles)
             nc.vector.tensor_tensor(
-                out=grouped[:].rearrange("p (n t) -> p n t", t=PACK),
+                out=grouped[:, slot * P * PACK : (slot * P + n) * PACK].rearrange("p (n t) -> p n t", t=PACK),
                 in0=pair.rearrange("p i x -> p (i x)").unsqueeze(2).to_broadcast([P, n, PACK]),
-                in1=a_reps[r][:, :, first * P : first * P + n].rearrange("p t n -> p n t"),
+                in1=a_rep[:, :, col : col + n].rearrange("p t n -> p n t"),
                 op=MULT,
             )
-            return grouped
 
-        def turn_words(kron_t, bank_tile):
+        def turn_words(kron_t):
             turned = psum.tile([P, BANK_TILES, 2, P], F32, tag="bank")
             for i in range(BANK_TILES):
                 for u in range(2):
-                    nc.tensor.transpose(turned[:, i, u, :], kron_t[:, bank_tile + i, u, :].bitcast(F32), ident_f32[:])
+                    nc.tensor.transpose(turned[:, i, u, :], kron_t[:, i, u, :].bitcast(F32), ident_f32[:])
             return turned
 
         def empty_words(engine_copy, turned, grouped, bank_tile):
@@ -198,19 +201,18 @@ def tile_fast_tucker_taylor_pa_s_kernel(tc, z, G2_words, G2_scales, out):
             engine_copy(out=result[:], in_=acc[:])
             nc.sync.dma_start(out=out[P * half : P * (half + 1), first * P : first * P + width], in_=result[:])
 
-        f_s, f_v, f_g = 6, 9, 14
-        n_s = 3
         V_COPY, S_COPY = nc.vector.tensor_copy, nc.scalar.copy
 
-        ba_t = keep.tile([P, n_s, 2, RANK * HE], F32)
-        for u in range(2):
-            nc.vector.tensor_tensor(
-                out=ba_t[:, :, u, :].rearrange("x j (b he) -> x j b he", he=HE),
-                in0=z1_of(f_s, n_s).unsqueeze(3).to_broadcast([P, n_s, RANK, HE]),
-                in1=z0_of(z_psum[:, 0, :], f_s, n_s, u).unsqueeze(2).to_broadcast([P, n_s, RANK, HE]),
-                op=MULT,
-            )
-        kron_t = keep.tile([P, 6, 2, K // 2], BF16)
+        def ba_products(first, n):
+            ba_t = work.tile([P, n, 2, RANK * HE], F32)
+            for u in range(2):
+                nc.vector.tensor_tensor(
+                    out=ba_t[:, :, u, :].rearrange("x j (b he) -> x j b he", he=HE),
+                    in0=z1_of(first, n).unsqueeze(3).to_broadcast([P, n, RANK, HE]),
+                    in1=z0_of(z_psum[:, 0, :], first, n, u).unsqueeze(2).to_broadcast([P, n, RANK, HE]),
+                    op=MULT,
+                )
+            return ba_t
 
         def bc_products(who, first, n=2):
             bc_t = work.tile([P, n, RANK * RANK], F32)
@@ -222,68 +224,79 @@ def tile_fast_tucker_taylor_pa_s_kernel(tc, z, G2_words, G2_scales, out):
             )
             return bc_t
 
-        def scalar_products():
-            for i in range(n_s):
+        def scalar_products(kron_t, slot, ba_t, ba_slot, first, n):
+            for i in range(n):
                 for c in range(RANK):
-                    col = c * N_TILES + f_s + i
+                    col = c * N_TILES + first + i
                     nc.scalar.activation(
-                        out=kron_t[:, i, :, RANK * HE * c : RANK * HE * (c + 1)],
-                        in_=ba_t[:, i, :, :],
+                        out=kron_t[:, slot + i, :, RANK * HE * c : RANK * HE * (c + 1)],
+                        in_=ba_t[:, ba_slot + i, :, :],
                         func=COPY,
                         scale=z2_f32[:, col : col + 1],
                     )
 
-        def sample_products(engine, z0_source, bc_t, slot, first, i, n):
+        def sample_products(engine, z0_source, kron_t, slot, bc_t, bc_slot, first, parts=1):
+            part = RANK * RANK // parts
             for u in range(2):
-                engine.tensor_tensor(
-                    out=kron_t[:, slot + i : slot + i + n, u, :].rearrange("x j (cb he) -> x j cb he", he=HE),
-                    in0=bc_t[:, i : i + n, :].unsqueeze(3).to_broadcast([P, n, RANK * RANK, HE]),
-                    in1=z0_of(z0_source, first + i, n, u).unsqueeze(2).to_broadcast([P, n, RANK * RANK, HE]),
-                    op=MULT,
-                )
+                for cb in range(0, RANK * RANK, part):
+                    engine.tensor_tensor(
+                        out=kron_t[:, slot, u, HE * cb : HE * (cb + part)].rearrange("x (cb he) -> x cb he", he=HE),
+                        in0=bc_t[:, bc_slot, cb : cb + part].unsqueeze(2).to_broadcast([P, part, HE]),
+                        in1=z0_of(z0_source, first, 1, u)[:, 0, :].unsqueeze(1).to_broadcast([P, part, HE]),
+                        op=MULT,
+                    )
 
-        grouped_x = big.tile([P, 4 * P * PACK], BF16, align_bytes=64, tag="grouped")
-        grouped_g = big.tile([P, 2 * P * PACK], BF16, align_bytes=64, tag="grouped")
-        scalar_products()
+        ba6 = ba_products(6, 3)
+        groupedS = big.tile([P, 4 * P * PACK], BF16, align_bytes=64, tag="grouped")
+        grouped0 = big.tile([P, 2 * P * PACK], BF16, align_bytes=64, tag="grouped")
+        grouped2 = big.tile([P, 4 * P * PACK], BF16, align_bytes=64, tag="grouped")
+        grouped10a = big.tile([P, 2 * P * PACK], BF16, align_bytes=64, tag="grouped")
+        grouped10b = big.tile([P, 2 * P * PACK], BF16, align_bytes=64, tag="grouped")
+        groupedGg = big.tile([P, 2 * P * PACK], BF16, align_bytes=64, tag="grouped")
+        kron_s0 = big.tile([P, 2, 2, K // 2], BF16, tag="kron")
+        kron_s1 = big.tile([P, 2, 2, K // 2], BF16, tag="kron")
+        kron_g = big.tile([P, 2, 2, K // 2], BF16, tag="kron")
+        scalar_products(kron_s0, 0, ba6, 0, 6, 2)
+        scalar_products(kron_s1, 0, ba6, 2, 8, 1)
         pair_t0 = pair_products("vector", 0, 2)
         pair0 = turn(pair_t0, 0, 2)
-        bc_v = bc_products("vector", f_v, 1)
-        sample_products(nc.vector, z_psum[:, 0, :], bc_v, 3, f_v, 0, 1)
-        pair_t1 = pair_products("gpsimd", 2, 4)
-        pair_t2 = pair_products("gpsimd", 10, 4)
-        bc_g = bc_products("gpsimd", f_g)
-        sample_products(nc.gpsimd, z0_sorted, bc_g, 4, f_g, 0, 1)
-        sample_products(nc.gpsimd, z0_sorted, bc_g, 4, f_g, 1, 1)
-        pair1 = turn(pair_t1, 0, 4)
-        words_s = turn_words(kron_t, 0)
-        words_v = turn_words(kron_t, 2)
-        empty_words(S_COPY, words_s, grouped_x, 0)
-        empty_words(S_COPY, words_v, grouped_x, 2)
-        grouped0 = last_products(pair0[:], 0)
+        bc9 = bc_products("vector", 9, 1)
+        sample_products(nc.vector, z_psum[:, 0, :], kron_s1, 1, bc9, 0, 9)
+        pair_t2 = pair_products("gpsimd", 2, 4)
+        pair_t10 = pair_products("gpsimd", 10, 4)
+        bc14 = bc_products("gpsimd", 14, 2)
+        sample_products(nc.gpsimd, z0_sorted, kron_g, 0, bc14, 0, 14, 1)
+        sample_products(nc.gpsimd, z0_sorted, kron_g, 1, bc14, 1, 15, 1)
         pair2 = turn(pair_t2, 0, 4)
-        grouped1 = last_products(pair1[:], 1)
+        words_s0 = turn_words(kron_s0)
+        empty_words(S_COPY, words_s0, groupedS, 0)
+        last_products(pair0[:, 0:2, :], 0, 2, grouped0, 0)
+        pair10 = turn(pair_t10, 0, 4)
+        words_s1 = turn_words(kron_s1)
+        empty_words(S_COPY, words_s1, groupedS, 2)
+        last_products(pair2[:, 0:4, :], 2, 4, grouped2, 0)
         q0 = quantise(grouped0[:], 256)
         acc0 = matmuls_one_bank(q0, 256)
         store_both(S_COPY, acc0, 0, 256)
-        qx = quantise(grouped_x[:], 512)
-        accx = matmuls(qx, 512)
-        store(S_COPY, accx[0], 0, f_s, 512)
-        store(S_COPY, accx[1], 1, f_s, 512)
-        q1 = quantise(grouped1[:], 512)
-        words_g = turn_words(kron_t, 4)
-        empty_words(S_COPY, words_g, grouped_g, 0)
-        acc1 = matmuls(q1, 512)
-        store(S_COPY, acc1[0], 0, 2, 512)
-        store(S_COPY, acc1[1], 1, 2, 512)
-        grouped2a = last_products(pair2[:, 0:2, :], 3, 0, 2)
-        grouped2b = last_products(pair2[:, 2:4, :], 3, 2, 2)
-        qg = quantise(grouped_g[:], 256)
-        accg = matmuls_one_bank(qg, 256)
-        store_both(S_COPY, accg, f_g, 256)
-        q2a = quantise(grouped2a[:], 256)
-        acc2a = matmuls_one_bank(q2a, 256)
-        q2b = quantise(grouped2b[:], 256)
-        store_both(V_COPY, acc2a, 10, 256)
-        acc2b = matmuls(q2b, 256)
-        store(S_COPY, acc2b[0], 0, 12, 256)
-        store(V_COPY, acc2b[1], 1, 12, 256)
+        q2 = quantise(grouped2[:], 512)
+        acc2 = matmuls(q2, 512)
+        last_products(pair10[:, 0:2, :], 10, 2, grouped10a, 0)
+        store(S_COPY, acc2[0], 0, 2, 512)
+        store(S_COPY, acc2[1], 1, 2, 512)
+        qS = quantise(groupedS[:], 512)
+        words_g = turn_words(kron_g)
+        empty_words(S_COPY, words_g, groupedGg, 0)
+        accS = matmuls(qS, 512)
+        store(S_COPY, accS[0], 0, 6, 512)
+        store(S_COPY, accS[1], 1, 6, 512)
+        last_products(pair10[:, 2:4, :], 12, 2, grouped10b, 0)
+        q10a = quantise(grouped10a[:], 256)
+        acc10a = matmuls_one_bank(q10a, 256)
+        store_both(S_COPY, acc10a, 10, 256)
+        qGg = quantise(groupedGg[:], 256)
+        accGg = matmuls_one_bank(qGg, 256)
+        q10b = quantise(grouped10b[:], 256)
+        store_both(V_COPY, accGg, 14, 256)
+        acc10b = matmuls(q10b, 256)
+        store(S_COPY, acc10b[0], 0, 12, 256)
+        store(V_COPY, acc10b[1], 1, 12, 256)

@@ -39,7 +39,8 @@ def tile_fast_tucker_taylor_pa_s_kernel(tc, z, G2_words, G2_scales, out):
         ctx.enter_context(tc.manual_schedule())
 
         z_rows = keep.tile([P, 3, P], BF16)
-        nc.sync.dma_start(out=z_rows[:], in_=z.rearrange("g a (j x) -> (a j) g x", x=P))
+        for g in (1, 2, 0):
+            nc.sync.dma_start(out=z_rows[:, g, :], in_=z[g].rearrange("a (j x) -> (a j) x", x=P))
 
         def load_a_rep(first, n_tiles):
             width = n_tiles * P
@@ -80,44 +81,54 @@ def tile_fast_tucker_taylor_pa_s_kernel(tc, z, G2_words, G2_scales, out):
         sort_flat = sort_ujhe[:].rearrange("v u y -> v (u y)")
         z1_psum = psum.tile([P, P], BF16, tag="bank")
         nc.tensor.transpose(z1_psum[:], z_rows[:, 1, :], ident_bf16[:])
-        z_scalar = psum.tile([P, 2, P], BF16, tag="bank")
-        nc.tensor.transpose(z_scalar[:, 1, :], z_rows[:, 2, :], ident_bf16[:])
-        nc.tensor.transpose(z_scalar[:, 0, :], z_rows[:, 0, :], sort_flat)
-        z_psum = psum.tile([P, 2, P], BF16, tag="bank")
-        nc.tensor.transpose(z_psum[:, 1, :], z_rows[:, 2, :], ident_bf16[:])
-        nc.tensor.transpose(z_psum[:, 0, :], z_rows[:, 0, :], sort_flat)
+        z2_psum = psum.tile([P, P], BF16, tag="bank")
+        nc.tensor.transpose(z2_psum[:], z_rows[:, 2, :], ident_bf16[:])
+        z0_psum = psum.tile([P, P], BF16, tag="bank")
+        nc.tensor.transpose(z0_psum[:], z_rows[:, 0, :], sort_flat)
+        z2_f32 = keep.tile([P, P], F32)
+        nc.scalar.copy(out=z2_f32[:], in_=z2_psum[:])
         z1h = keep.tile([P, N_TILES, BH], BF16)
-        nc.vector.tensor_copy(
+        nc.scalar.copy(
             out=z1h[:].rearrange("x j (b h) -> x j b h", h=2),
             in_=z1_psum[:].rearrange("x (b j) -> x j b", b=RANK).unsqueeze(3).to_broadcast([P, N_TILES, RANK, 2]),
         )
-        z2_f32 = keep.tile([P, P], F32)
-        nc.scalar.copy(out=z2_f32[:], in_=z_scalar[:, 1, :])
         z0_sorted = keep.tile([P, P], BF16)
-        nc.scalar.copy(out=z0_sorted[:], in_=z_scalar[:, 0, :])
+        nc.scalar.copy(out=z0_sorted[:], in_=z0_psum[:])
 
-        def z1_of(first, n_tiles):
-            return z1h[:, first : first + n_tiles, :].rearrange("x j (b h) -> x j b h", h=2)[:, :, :, 0]
+        def rows_of(source, first, n_tiles):
+            return source.rearrange("x (r j) -> x j r", r=RANK)[:, first : first + n_tiles, :]
 
         engines = {"vector": nc.vector, "gpsimd": nc.gpsimd}
-        z2_sources = {"vector": z_psum[:, 1, :], "gpsimd": z2_f32[:]}
 
-        def z2_of(who, first, n_tiles):
-            return z2_sources[who].rearrange("x (c j) -> x j c", c=RANK)[:, first : first + n_tiles, :]
+        def z1_of(who, first, n_tiles):
+            if who == "vector":
+                return rows_of(z1_psum[:], first, n_tiles)
+            return z1h[:, first : first + n_tiles, :].rearrange("x j (b h) -> x j b h", h=2)[:, :, :, 0]
 
         def z0_of(source, first, n_tiles, u):
             start = u * (P // 2) + first * HE
             return source[:, start : start + n_tiles * HE].rearrange("x (j he) -> x j he", he=HE)
 
         def pair_products(who, first, n_tiles):
-            shape = [P, n_tiles, RANK, BH]
             pair_t = work.tile([P, n_tiles, P], F32)
-            engines[who].tensor_tensor(
-                out=pair_t[:].rearrange("x j (c bh) -> x j c bh", bh=BH),
-                in0=z2_of(who, first, n_tiles).unsqueeze(3).to_broadcast(shape),
-                in1=z1h[:, first : first + n_tiles, :].unsqueeze(2).to_broadcast(shape),
-                op=MULT,
-            )
+            z2 = rows_of(z2_f32[:], first, n_tiles)
+            if who == "gpsimd":
+                shape = [P, n_tiles, RANK, BH]
+                nc.gpsimd.tensor_tensor(
+                    out=pair_t[:].rearrange("x j (c bh) -> x j c bh", bh=BH),
+                    in0=z2.unsqueeze(3).to_broadcast(shape),
+                    in1=z1h[:, first : first + n_tiles, :].unsqueeze(2).to_broadcast(shape),
+                    op=MULT,
+                )
+                return pair_t
+            shape = [P, RANK, RANK, 2]
+            for i in range(n_tiles):
+                nc.vector.tensor_tensor(
+                    out=pair_t[:, i, :].rearrange("x (c b h) -> x c b h", b=RANK, h=2),
+                    in0=z2[:, i, :].unsqueeze(2).unsqueeze(3).to_broadcast(shape),
+                    in1=rows_of(z1_psum[:], first + i, 1)[:, 0, :].unsqueeze(1).unsqueeze(3).to_broadcast(shape),
+                    op=MULT,
+                )
             return pair_t
 
         def next_a(first, n_tiles):
@@ -208,8 +219,8 @@ def tile_fast_tucker_taylor_pa_s_kernel(tc, z, G2_words, G2_scales, out):
             for u in range(2):
                 nc.vector.tensor_tensor(
                     out=ba_t[:, :, u, :].rearrange("x j (b he) -> x j b he", he=HE),
-                    in0=z1_of(first, n).unsqueeze(3).to_broadcast([P, n, RANK, HE]),
-                    in1=z0_of(z_psum[:, 0, :], first, n, u).unsqueeze(2).to_broadcast([P, n, RANK, HE]),
+                    in0=z1_of("gpsimd", first, n).unsqueeze(3).to_broadcast([P, n, RANK, HE]),
+                    in1=z0_of(z0_psum[:], first, n, u).unsqueeze(2).to_broadcast([P, n, RANK, HE]),
                     op=MULT,
                 )
             return ba_t
@@ -218,8 +229,8 @@ def tile_fast_tucker_taylor_pa_s_kernel(tc, z, G2_words, G2_scales, out):
             bc_t = work.tile([P, n, RANK * RANK], F32)
             engines[who].tensor_tensor(
                 out=bc_t[:].rearrange("x j (c b) -> x j c b", b=RANK),
-                in0=z2_of(who, first, n).unsqueeze(3).to_broadcast([P, n, RANK, RANK]),
-                in1=z1_of(first, n).unsqueeze(2).to_broadcast([P, n, RANK, RANK]),
+                in0=rows_of(z2_f32[:], first, n).unsqueeze(3).to_broadcast([P, n, RANK, RANK]),
+                in1=z1_of(who, first, n).unsqueeze(2).to_broadcast([P, n, RANK, RANK]),
                 op=MULT,
             )
             return bc_t
@@ -246,7 +257,6 @@ def tile_fast_tucker_taylor_pa_s_kernel(tc, z, G2_words, G2_scales, out):
                         op=MULT,
                     )
 
-        ba6 = ba_products(6, 3)
         groupedS = big.tile([P, 4 * P * PACK], BF16, align_bytes=64, tag="grouped")
         grouped0 = big.tile([P, 2 * P * PACK], BF16, align_bytes=64, tag="grouped")
         grouped2 = big.tile([P, 4 * P * PACK], BF16, align_bytes=64, tag="grouped")
@@ -256,12 +266,13 @@ def tile_fast_tucker_taylor_pa_s_kernel(tc, z, G2_words, G2_scales, out):
         kron_s0 = big.tile([P, 2, 2, K // 2], BF16, tag="kron")
         kron_s1 = big.tile([P, 2, 2, K // 2], BF16, tag="kron")
         kron_g = big.tile([P, 2, 2, K // 2], BF16, tag="kron")
-        scalar_products(kron_s0, 0, ba6, 0, 6, 2)
-        scalar_products(kron_s1, 0, ba6, 2, 8, 1)
         pair_t0 = pair_products("vector", 0, 2)
         pair0 = turn(pair_t0, 0, 2)
+        ba6 = ba_products(6, 3)
+        scalar_products(kron_s0, 0, ba6, 0, 6, 2)
+        scalar_products(kron_s1, 0, ba6, 2, 8, 1)
         bc9 = bc_products("vector", 9, 1)
-        sample_products(nc.vector, z_psum[:, 0, :], kron_s1, 1, bc9, 0, 9)
+        sample_products(nc.vector, z0_psum[:], kron_s1, 1, bc9, 0, 9)
         pair_t2 = pair_products("gpsimd", 2, 4)
         pair_t10 = pair_products("gpsimd", 10, 4)
         bc14 = bc_products("gpsimd", 14, 2)

@@ -17,7 +17,6 @@ P = 128
 PACK = 4
 RANK = 8
 BH = 2 * RANK
-HE = RANK // 2
 K = RANK * RANK * RANK
 SAMPLES = 2048
 N_TILES = SAMPLES // P
@@ -35,7 +34,8 @@ def tile_fast_tucker_taylor_pa_s_kernel(tc, z, G2_words, G2_scales, out):
         work = ctx.enter_context(tc.tile_pool(name="work", bufs=8))
         big = ctx.enter_context(tc.tile_pool(name="big", bufs=8))
         stage = ctx.enter_context(tc.tile_pool(name="stage", bufs=16))
-        psum = ctx.enter_context(tc.psum_pool(name="psum", bufs=8))
+        psum_turn = ctx.enter_context(tc.psum_pool(name="psum_turn", bufs=4))
+        psum = ctx.enter_context(tc.psum_pool(name="psum", bufs=4))
         ctx.enter_context(tc.manual_schedule())
 
         z_rows = keep.tile([P, 3, P], BF16)
@@ -52,13 +52,7 @@ def tile_fast_tucker_taylor_pa_s_kernel(tc, z, G2_words, G2_scales, out):
                 )
             return a_rep
 
-        a_reps = {}
-        for first, n_tiles in LOADS[:2]:
-            a_reps[first, n_tiles] = load_a_rep(first, n_tiles)
-        w_words = keep.tile([P, 2 * OUT_ROWS], U8, align_bytes=64)
-        nc.sync.dma_start(out=w_words[:].bitcast(I32), in_=G2_words[0].bitcast(I32))
-        for first, n_tiles in LOADS[2:]:
-            a_reps[first, n_tiles] = load_a_rep(first, n_tiles)
+        a_reps = {LOADS[0]: load_a_rep(*LOADS[0])}
         w_scales = keep.tile([P, OUT_ROWS], U8, align_bytes=64)
         nc.vector.memset(w_scales[:].bitcast(I32), 0)
         for quad in range(4):
@@ -66,25 +60,27 @@ def tile_fast_tucker_taylor_pa_s_kernel(tc, z, G2_words, G2_scales, out):
                 out=w_scales[32 * quad : 32 * quad + 4, :].bitcast(I32),
                 in_=G2_scales[0, 4 * quad : 4 * quad + 4, :].bitcast(I32),
             )
+        w_words = keep.tile([P, 2 * OUT_ROWS], U8, align_bytes=64)
+        nc.sync.dma_start(out=w_words[:].bitcast(I32), in_=G2_words[0].bitcast(I32))
+        for first, n_tiles in LOADS[1:]:
+            a_reps[first, n_tiles] = load_a_rep(first, n_tiles)
 
         ident_bf16 = keep.tile([P, P], BF16)
         make_identity(nc, ident_bf16[:])
         ident_f32 = keep.tile([P, P], F32)
         make_identity(nc, ident_f32[:])
-        sort_ujhe = keep.tile([P, 2, P // 2], BF16)
-        for u in range(2):
-            nc.vector.tensor_copy(
-                out=sort_ujhe[:, u, :].rearrange("v (j h e) -> v j h e", h=2, e=2),
-                in_=ident_bf16[:].rearrange("v (h u e j) -> v u j h e", h=2, u=2, e=2)[:, u, :, :, :],
-            )
+        sort_ja = keep.tile([P, P], BF16)
+        nc.vector.tensor_copy(
+            out=sort_ja[:].rearrange("v (j a) -> v j a", a=RANK),
+            in_=ident_bf16[:].rearrange("v (a j) -> v j a", a=RANK),
+        )
 
-        sort_flat = sort_ujhe[:].rearrange("v u y -> v (u y)")
         z1_psum = psum.tile([P, P], BF16, tag="bank")
         nc.tensor.transpose(z1_psum[:], z_rows[:, 1, :], ident_bf16[:])
         z2_psum = psum.tile([P, P], BF16, tag="bank")
         nc.tensor.transpose(z2_psum[:], z_rows[:, 2, :], ident_bf16[:])
         z0_psum = psum.tile([P, P], BF16, tag="bank")
-        nc.tensor.transpose(z0_psum[:], z_rows[:, 0, :], sort_flat)
+        nc.tensor.transpose(z0_psum[:], z_rows[:, 0, :], sort_ja[:])
         z2_f32 = keep.tile([P, P], F32)
         nc.scalar.copy(out=z2_f32[:], in_=z2_psum[:])
         z1h = keep.tile([P, N_TILES, BH], BF16)
@@ -105,9 +101,8 @@ def tile_fast_tucker_taylor_pa_s_kernel(tc, z, G2_words, G2_scales, out):
                 return rows_of(z1_psum[:], first, n_tiles)
             return z1h[:, first : first + n_tiles, :].rearrange("x j (b h) -> x j b h", h=2)[:, :, :, 0]
 
-        def z0_of(source, first, n_tiles, u):
-            start = u * (P // 2) + first * HE
-            return source[:, start : start + n_tiles * HE].rearrange("x (j he) -> x j he", he=HE)
+        def z0_of(source, first, n_tiles):
+            return source[:, RANK * first : RANK * (first + n_tiles)].rearrange("x (j a) -> x j a", a=RANK)
 
         def pair_products(who, first, n_tiles):
             pair_t = work.tile([P, n_tiles, P], F32)
@@ -137,7 +132,7 @@ def tile_fast_tucker_taylor_pa_s_kernel(tc, z, G2_words, G2_scales, out):
                     return a_reps[start, tiles], (first - start) * P
 
         def turn(pair_t, first, n_tiles):
-            pair = psum.tile([P, n_tiles, P], F32, tag="bank")
+            pair = psum_turn.tile([P, n_tiles, P], F32, tag="bank")
             for i in range(n_tiles):
                 nc.tensor.transpose(pair[:, i, :], pair_t[:, first + i, :], ident_f32[:])
             return pair
@@ -153,10 +148,10 @@ def tile_fast_tucker_taylor_pa_s_kernel(tc, z, G2_words, G2_scales, out):
             )
 
         def turn_words(kron_t):
-            turned = psum.tile([P, BANK_TILES, 2, P], F32, tag="bank")
+            turned = psum_turn.tile([P, BANK_TILES, 2, P], F32, tag="bank")
             for i in range(BANK_TILES):
                 for u in range(2):
-                    nc.tensor.transpose(turned[:, i, u, :], kron_t[:, i, u, :].bitcast(F32), ident_f32[:])
+                    nc.tensor.transpose(turned[:, i, u, :], kron_t[:, i, :].bitcast(F32)[:, u : K // 2 : 2], ident_f32[:])
             return turned
 
         def empty_words(engine_copy, turned, grouped, bank_tile):
@@ -215,14 +210,13 @@ def tile_fast_tucker_taylor_pa_s_kernel(tc, z, G2_words, G2_scales, out):
         V_COPY, S_COPY = nc.vector.tensor_copy, nc.scalar.copy
 
         def ba_products(first, n):
-            ba_t = work.tile([P, n, 2, RANK * HE], F32)
-            for u in range(2):
-                nc.vector.tensor_tensor(
-                    out=ba_t[:, :, u, :].rearrange("x j (b he) -> x j b he", he=HE),
-                    in0=z1_of("gpsimd", first, n).unsqueeze(3).to_broadcast([P, n, RANK, HE]),
-                    in1=z0_of(z0_psum[:], first, n, u).unsqueeze(2).to_broadcast([P, n, RANK, HE]),
-                    op=MULT,
-                )
+            ba_t = work.tile([P, n, RANK * RANK], F32)
+            nc.vector.tensor_tensor(
+                out=ba_t[:].rearrange("x j (b a) -> x j b a", a=RANK),
+                in0=z1_of("gpsimd", first, n).unsqueeze(3).to_broadcast([P, n, RANK, RANK]),
+                in1=z0_of(z0_psum[:], first, n).unsqueeze(2).to_broadcast([P, n, RANK, RANK]),
+                op=MULT,
+            )
             return ba_t
 
         def bc_products(who, first, n=2):
@@ -240,22 +234,21 @@ def tile_fast_tucker_taylor_pa_s_kernel(tc, z, G2_words, G2_scales, out):
                 for c in range(RANK):
                     col = c * N_TILES + first + i
                     nc.scalar.activation(
-                        out=kron_t[:, slot + i, :, RANK * HE * c : RANK * HE * (c + 1)],
-                        in_=ba_t[:, ba_slot + i, :, :],
+                        out=kron_t[:, slot + i, RANK * RANK * c : RANK * RANK * (c + 1)],
+                        in_=ba_t[:, ba_slot + i, :],
                         func=COPY,
                         scale=z2_f32[:, col : col + 1],
                     )
 
         def sample_products(engine, z0_source, kron_t, slot, bc_t, bc_slot, first, parts=1):
             part = RANK * RANK // parts
-            for u in range(2):
-                for cb in range(0, RANK * RANK, part):
-                    engine.tensor_tensor(
-                        out=kron_t[:, slot, u, HE * cb : HE * (cb + part)].rearrange("x (cb he) -> x cb he", he=HE),
-                        in0=bc_t[:, bc_slot, cb : cb + part].unsqueeze(2).to_broadcast([P, part, HE]),
-                        in1=z0_of(z0_source, first, 1, u)[:, 0, :].unsqueeze(1).to_broadcast([P, part, HE]),
-                        op=MULT,
-                    )
+            for cb in range(0, RANK * RANK, part):
+                engine.tensor_tensor(
+                    out=kron_t[:, slot, RANK * cb : RANK * (cb + part)].rearrange("x (cb a) -> x cb a", a=RANK),
+                    in0=bc_t[:, bc_slot, cb : cb + part].unsqueeze(2).to_broadcast([P, part, RANK]),
+                    in1=z0_of(z0_source, first, 1)[:, 0, :].unsqueeze(1).to_broadcast([P, part, RANK]),
+                    op=MULT,
+                )
 
         groupedS = big.tile([P, 4 * P * PACK], BF16, align_bytes=64, tag="grouped")
         grouped0 = big.tile([P, 2 * P * PACK], BF16, align_bytes=64, tag="grouped")
@@ -263,9 +256,9 @@ def tile_fast_tucker_taylor_pa_s_kernel(tc, z, G2_words, G2_scales, out):
         grouped10a = big.tile([P, 2 * P * PACK], BF16, align_bytes=64, tag="grouped")
         grouped10b = big.tile([P, 2 * P * PACK], BF16, align_bytes=64, tag="grouped")
         groupedGg = big.tile([P, 2 * P * PACK], BF16, align_bytes=64, tag="grouped")
-        kron_s0 = big.tile([P, 2, 2, K // 2], BF16, tag="kron")
-        kron_s1 = big.tile([P, 2, 2, K // 2], BF16, tag="kron")
-        kron_g = big.tile([P, 2, 2, K // 2], BF16, tag="kron")
+        kron_s0 = big.tile([P, 2, K], BF16, tag="kron")
+        kron_s1 = big.tile([P, 2, K], BF16, tag="kron")
+        kron_g = big.tile([P, 2, K], BF16, tag="kron")
         pair_t0 = pair_products("vector", 0, 2)
         pair0 = turn(pair_t0, 0, 2)
         ba6 = ba_products(6, 3)
@@ -273,19 +266,22 @@ def tile_fast_tucker_taylor_pa_s_kernel(tc, z, G2_words, G2_scales, out):
         scalar_products(kron_s1, 0, ba6, 2, 8, 1)
         bc9 = bc_products("vector", 9, 1)
         sample_products(nc.vector, z0_psum[:], kron_s1, 1, bc9, 0, 9)
-        pair_t2 = pair_products("gpsimd", 2, 4)
+        pair_t2 = pair_products("gpsimd", 2, 2)
+        pair_t4 = pair_products("gpsimd", 4, 2)
         pair_t10 = pair_products("gpsimd", 10, 4)
         bc14 = bc_products("gpsimd", 14, 2)
-        sample_products(nc.gpsimd, z0_sorted, kron_g, 0, bc14, 0, 14, 1)
-        sample_products(nc.gpsimd, z0_sorted, kron_g, 1, bc14, 1, 15, 1)
-        pair2 = turn(pair_t2, 0, 4)
+        sample_products(nc.gpsimd, z0_sorted, kron_g, 0, bc14, 0, 14, 2)
+        sample_products(nc.gpsimd, z0_sorted, kron_g, 1, bc14, 1, 15, 2)
+        pair2 = turn(pair_t2, 0, 2)
+        pair4 = turn(pair_t4, 0, 2)
         words_s0 = turn_words(kron_s0)
         empty_words(S_COPY, words_s0, groupedS, 0)
         last_products(pair0[:, 0:2, :], 0, 2, grouped0, 0)
         pair10 = turn(pair_t10, 0, 4)
+        last_products(pair2[:], 2, 2, grouped2, 0)
         words_s1 = turn_words(kron_s1)
         empty_words(S_COPY, words_s1, groupedS, 2)
-        last_products(pair2[:, 0:4, :], 2, 4, grouped2, 0)
+        last_products(pair4[:], 4, 2, grouped2, 2)
         q0 = quantise(grouped0[:], 256)
         acc0 = matmuls_one_bank(q0, 256)
         store_both(S_COPY, acc0, 0, 256)
@@ -300,14 +296,15 @@ def tile_fast_tucker_taylor_pa_s_kernel(tc, z, G2_words, G2_scales, out):
         accS = matmuls(qS, 512)
         store(S_COPY, accS[0], 0, 6, 512)
         store(S_COPY, accS[1], 1, 6, 512)
-        last_products(pair10[:, 2:4, :], 12, 2, grouped10b, 0)
         q10a = quantise(grouped10a[:], 256)
         acc10a = matmuls_one_bank(q10a, 256)
         store_both(S_COPY, acc10a, 10, 256)
+        last_products(pair10[:, 2:4, :], 12, 2, grouped10b, 0)
         qGg = quantise(groupedGg[:], 256)
-        accGg = matmuls_one_bank(qGg, 256)
+        accGg = matmuls(qGg, 256)
         q10b = quantise(grouped10b[:], 256)
-        store_both(V_COPY, accGg, 14, 256)
+        store(V_COPY, accGg[0], 0, 14, 256)
+        store(S_COPY, accGg[1], 1, 14, 256)
         acc10b = matmuls(q10b, 256)
         store(S_COPY, acc10b[0], 0, 12, 256)
         store(V_COPY, acc10b[1], 1, 12, 256)

@@ -22,7 +22,7 @@ SAMPLES = 2048
 N_TILES = SAMPLES // P
 OUT_ROWS = 256
 BANK_TILES = 2
-LOADS = ((0, 2), (2, 4), (10, 4))
+LOADS = ((0, 4), (10, 4))
 
 FLOPS = 2 * OUT_ROWS * K * SAMPLES
 
@@ -34,8 +34,7 @@ def tile_fast_tucker_taylor_pa_s_kernel(tc, z, G2_words, G2_scales, out):
         work = ctx.enter_context(tc.tile_pool(name="work", bufs=8))
         big = ctx.enter_context(tc.tile_pool(name="big", bufs=8))
         stage = ctx.enter_context(tc.tile_pool(name="stage", bufs=16))
-        psum_turn = ctx.enter_context(tc.psum_pool(name="psum_turn", bufs=4))
-        psum = ctx.enter_context(tc.psum_pool(name="psum", bufs=4))
+        psum = ctx.enter_context(tc.psum_pool(name="psum", bufs=1))
         ctx.enter_context(tc.manual_schedule())
 
         z_rows = keep.tile([P, 3, P], BF16)
@@ -75,11 +74,11 @@ def tile_fast_tucker_taylor_pa_s_kernel(tc, z, G2_words, G2_scales, out):
             in_=ident_bf16[:].rearrange("v (a j) -> v j a", a=RANK),
         )
 
-        z1_psum = psum.tile([P, P], BF16, tag="bank")
+        z1_psum = psum.tile([P, P], BF16, tag="b0")
         nc.tensor.transpose(z1_psum[:], z_rows[:, 1, :], ident_bf16[:])
-        z2_psum = psum.tile([P, P], BF16, tag="bank")
+        z2_psum = psum.tile([P, P], BF16, tag="b1")
         nc.tensor.transpose(z2_psum[:], z_rows[:, 2, :], ident_bf16[:])
-        z0_psum = psum.tile([P, P], BF16, tag="bank")
+        z0_psum = psum.tile([P, P], BF16, tag="b2")
         nc.tensor.transpose(z0_psum[:], z_rows[:, 0, :], sort_ja[:])
         z2_f32 = keep.tile([P, P], F32)
         nc.scalar.copy(out=z2_f32[:], in_=z2_psum[:])
@@ -131,8 +130,8 @@ def tile_fast_tucker_taylor_pa_s_kernel(tc, z, G2_words, G2_scales, out):
                 if start <= first and first + n_tiles <= start + tiles:
                     return a_reps[start, tiles], (first - start) * P
 
-        def turn(pair_t, first, n_tiles):
-            pair = psum_turn.tile([P, n_tiles, P], F32, tag="bank")
+        def turn(pair_t, first, n_tiles, bank):
+            pair = psum.tile([P, n_tiles, P], F32, tag=bank)
             for i in range(n_tiles):
                 nc.tensor.transpose(pair[:, i, :], pair_t[:, first + i, :], ident_f32[:])
             return pair
@@ -147,8 +146,8 @@ def tile_fast_tucker_taylor_pa_s_kernel(tc, z, G2_words, G2_scales, out):
                 op=MULT,
             )
 
-        def turn_words(kron_t):
-            turned = psum_turn.tile([P, BANK_TILES, 2, P], F32, tag="bank")
+        def turn_words(kron_t, bank):
+            turned = psum.tile([P, BANK_TILES, 2, P], F32, tag=bank)
             for i in range(BANK_TILES):
                 for u in range(2):
                     nc.tensor.transpose(turned[:, i, u, :], kron_t[:, i, :].bitcast(F32)[:, u : K // 2 : 2], ident_f32[:])
@@ -167,10 +166,10 @@ def tile_fast_tucker_taylor_pa_s_kernel(tc, z, G2_words, G2_scales, out):
             nc.vector.quantize_mx(out=codes[:].bitcast(FP8X4), scales=scales[:], in_=grouped_cols)
             return codes, scales
 
-        def matmuls(quantised, width):
+        def matmuls(quantised, width, banks):
             accs = []
             for half in range(OUT_ROWS // P):
-                acc = psum.tile([P, width], F32, tag="bank")
+                acc = psum.tile([P, width], F32, tag=banks[half])
                 nc.tensor.matmul_mx(
                     out=acc[:],
                     lhsT=w_words[:, 2 * P * half : 2 * P * (half + 1)].bitcast(FP4X4),
@@ -183,8 +182,8 @@ def tile_fast_tucker_taylor_pa_s_kernel(tc, z, G2_words, G2_scales, out):
                 accs.append(acc)
             return accs
 
-        def matmuls_one_bank(quantised, width):
-            acc = psum.tile([P, OUT_ROWS // P, width], F32, tag="bank")
+        def matmuls_one_bank(quantised, width, bank):
+            acc = psum.tile([P, OUT_ROWS // P, width], F32, tag=bank)
             for half in range(OUT_ROWS // P):
                 nc.tensor.matmul_mx(
                     out=acc[:, half, :],
@@ -250,61 +249,63 @@ def tile_fast_tucker_taylor_pa_s_kernel(tc, z, G2_words, G2_scales, out):
                     op=MULT,
                 )
 
+        groupedV = big.tile([P, 2 * P * PACK], BF16, align_bytes=64, tag="grouped")
+        grouped0 = big.tile([P, 4 * P * PACK], BF16, align_bytes=64, tag="grouped")
         groupedS = big.tile([P, 4 * P * PACK], BF16, align_bytes=64, tag="grouped")
-        grouped0 = big.tile([P, 2 * P * PACK], BF16, align_bytes=64, tag="grouped")
-        grouped2 = big.tile([P, 4 * P * PACK], BF16, align_bytes=64, tag="grouped")
         grouped10a = big.tile([P, 2 * P * PACK], BF16, align_bytes=64, tag="grouped")
         grouped10b = big.tile([P, 2 * P * PACK], BF16, align_bytes=64, tag="grouped")
         groupedGg = big.tile([P, 2 * P * PACK], BF16, align_bytes=64, tag="grouped")
+        kron_v = big.tile([P, 2, K], BF16, tag="kron")
         kron_s0 = big.tile([P, 2, K], BF16, tag="kron")
         kron_s1 = big.tile([P, 2, K], BF16, tag="kron")
         kron_g = big.tile([P, 2, K], BF16, tag="kron")
-        pair_t0 = pair_products("vector", 0, 2)
-        pair0 = turn(pair_t0, 0, 2)
-        ba6 = ba_products(6, 3)
-        scalar_products(kron_s0, 0, ba6, 0, 6, 2)
-        scalar_products(kron_s1, 0, ba6, 2, 8, 1)
-        bc9 = bc_products("vector", 9, 1)
-        sample_products(nc.vector, z0_psum[:], kron_s1, 1, bc9, 0, 9)
+        ba4 = ba_products(4, 3)
+        scalar_products(kron_s0, 0, ba4, 0, 4, 2)
+        bc7 = bc_products("vector", 7, 3)
+        sample_products(nc.vector, z0_psum[:], kron_v, 0, bc7, 1, 8)
+        sample_products(nc.vector, z0_psum[:], kron_v, 1, bc7, 2, 9)
+        sample_products(nc.vector, z0_psum[:], kron_s1, 1, bc7, 0, 7)
+        pair_t0 = pair_products("gpsimd", 0, 2)
         pair_t2 = pair_products("gpsimd", 2, 2)
-        pair_t4 = pair_products("gpsimd", 4, 2)
         pair_t10 = pair_products("gpsimd", 10, 4)
         bc14 = bc_products("gpsimd", 14, 2)
         sample_products(nc.gpsimd, z0_sorted, kron_g, 0, bc14, 0, 14, 2)
         sample_products(nc.gpsimd, z0_sorted, kron_g, 1, bc14, 1, 15, 2)
-        pair2 = turn(pair_t2, 0, 2)
-        pair4 = turn(pair_t4, 0, 2)
-        words_s0 = turn_words(kron_s0)
-        empty_words(S_COPY, words_s0, groupedS, 0)
+        pair0 = turn(pair_t0, 0, 2, "b3")
+        pair2 = turn(pair_t2, 0, 2, "b4")
+        words_v = turn_words(kron_v, "b5")
+        empty_words(S_COPY, words_v, groupedV, 0)
+        scalar_products(kron_s1, 0, ba4, 2, 6, 1)
         last_products(pair0[:, 0:2, :], 0, 2, grouped0, 0)
-        pair10 = turn(pair_t10, 0, 4)
-        last_products(pair2[:], 2, 2, grouped2, 0)
-        words_s1 = turn_words(kron_s1)
+        words_s0 = turn_words(kron_s0, "b6")
+        empty_words(S_COPY, words_s0, groupedS, 0)
+        pair10 = turn(pair_t10, 0, 4, "b3")
+        last_products(pair2[:, 0:2, :], 2, 2, grouped0, 2)
+        qV = quantise(groupedV[:], 256)
+        words_s1 = turn_words(kron_s1, "b7")
+        accV = matmuls_one_bank(qV, 256, "b0")
         empty_words(S_COPY, words_s1, groupedS, 2)
-        last_products(pair4[:], 4, 2, grouped2, 2)
-        q0 = quantise(grouped0[:], 256)
-        acc0 = matmuls_one_bank(q0, 256)
-        store_both(S_COPY, acc0, 0, 256)
-        q2 = quantise(grouped2[:], 512)
-        acc2 = matmuls(q2, 512)
+        store_both(S_COPY, accV, 8, 256)
+        q0 = quantise(grouped0[:], 512)
+        acc0 = matmuls(q0, 512, ("b1", "b5"))
         last_products(pair10[:, 0:2, :], 10, 2, grouped10a, 0)
-        store(S_COPY, acc2[0], 0, 2, 512)
-        store(S_COPY, acc2[1], 1, 2, 512)
+        store(S_COPY, acc0[0], 0, 0, 512)
+        store(S_COPY, acc0[1], 1, 0, 512)
         qS = quantise(groupedS[:], 512)
-        words_g = turn_words(kron_g)
+        words_g = turn_words(kron_g, "b7")
         empty_words(S_COPY, words_g, groupedGg, 0)
-        accS = matmuls(qS, 512)
-        store(S_COPY, accS[0], 0, 6, 512)
-        store(S_COPY, accS[1], 1, 6, 512)
+        accS = matmuls(qS, 512, ("b4", "b6"))
+        store(S_COPY, accS[0], 0, 4, 512)
+        store(S_COPY, accS[1], 1, 4, 512)
         q10a = quantise(grouped10a[:], 256)
-        acc10a = matmuls_one_bank(q10a, 256)
+        acc10a = matmuls_one_bank(q10a, 256, "b2")
         store_both(S_COPY, acc10a, 10, 256)
         last_products(pair10[:, 2:4, :], 12, 2, grouped10b, 0)
         qGg = quantise(groupedGg[:], 256)
-        accGg = matmuls(qGg, 256)
+        accGg = matmuls(qGg, 256, ("b0", "b5"))
         q10b = quantise(grouped10b[:], 256)
         store(V_COPY, accGg[0], 0, 14, 256)
         store(S_COPY, accGg[1], 1, 14, 256)
-        acc10b = matmuls(q10b, 256)
+        acc10b = matmuls(q10b, 256, ("b1", "b7"))
         store(S_COPY, acc10b[0], 0, 12, 256)
         store(V_COPY, acc10b[1], 1, 12, 256)

from contextlib import ExitStack

import concourse.mybir as mybir
from concourse.masks import make_identity

BF16 = mybir.dt.bfloat16
F32 = mybir.dt.float32
I32 = mybir.dt.int32
U8 = mybir.dt.uint8
U32 = mybir.dt.uint32
FP8X4 = mybir.dt.float8_e4m3fn_x4
FP4X4 = mybir.dt.float4_e2m1fn_x4
MULT = mybir.AluOpType.mult
COPY = mybir.ActivationFunctionType.Copy

P = 128
PACK = 4
RANK = 8
BH = 2 * RANK
K = RANK * RANK * RANK
SAMPLES = 2048
N_TILES = SAMPLES // P
OUT_ROWS = 256
BANK_TILES = 2
LOADS = ((0, 4), (10, 4))

FLOPS = 2 * OUT_ROWS * K * SAMPLES


def tile_fast_tucker_taylor_pa_s_kernel(tc, z, G2_words, G2_scales, out):
    nc = tc.nc
    with ExitStack() as ctx:
        keep = ctx.enter_context(tc.tile_pool(name="keep", bufs=1))
        work = ctx.enter_context(tc.tile_pool(name="work", bufs=8))
        big = ctx.enter_context(tc.tile_pool(name="big", bufs=8))
        stage = ctx.enter_context(tc.tile_pool(name="stage", bufs=16))
        psum = ctx.enter_context(tc.psum_pool(name="psum", bufs=1))
        ctx.enter_context(tc.manual_schedule())

        z_rows = keep.tile([P, 3, P], BF16)
        for g in (1, 2, 0):
            nc.sync.dma_start(out=z_rows[:, g, :], in_=z[g].rearrange("a (j x) -> (a j) x", x=P))

        def load_a_rep(first, n_tiles):
            width = n_tiles * P
            cols = slice(first * P, first * P + width)
            a_rep = work.tile([P, PACK, width], BF16)
            for h in range(2):
                nc.sync.dma_start(
                    out=a_rep[h:P:2, :, :], in_=z[0, PACK * h : PACK * (h + 1), cols].partition_broadcast(P // 2)
                )
            return a_rep

        a_reps = {LOADS[0]: load_a_rep(*LOADS[0])}
        w_scales = keep.tile([P, OUT_ROWS], U8, align_bytes=64)
        nc.vector.memset(w_scales[:].bitcast(I32), 0)
        for quad in range(4):
            nc.sync.dma_start(
                out=w_scales[32 * quad : 32 * quad + 4, :].bitcast(I32),
                in_=G2_scales[0, 4 * quad : 4 * quad + 4, :].bitcast(I32),
            )
        w_words = keep.tile([P, 2 * OUT_ROWS], U8, align_bytes=64)
        nc.sync.dma_start(out=w_words[:].bitcast(I32), in_=G2_words[0].bitcast(I32))
        for first, n_tiles in LOADS[1:]:
            a_reps[first, n_tiles] = load_a_rep(first, n_tiles)

        ident_bf16 = keep.tile([P, P], BF16)
        make_identity(nc, ident_bf16[:])
        ident_f32 = keep.tile([P, P], F32)
        make_identity(nc, ident_f32[:])
        sort_ja = keep.tile([P, P], BF16)
        nc.vector.tensor_copy(
            out=sort_ja[:].rearrange("v (j a) -> v j a", a=RANK),
            in_=ident_bf16[:].rearrange("v (a j) -> v j a", a=RANK),
        )

        z1_psum = psum.tile([P, P], BF16, tag="b0")
        nc.tensor.transpose(z1_psum[:], z_rows[:, 1, :], ident_bf16[:])
        z2_psum = psum.tile([P, P], BF16, tag="b1")
        nc.tensor.transpose(z2_psum[:], z_rows[:, 2, :], ident_bf16[:])
        z0_psum = psum.tile([P, P], BF16, tag="b2")
        nc.tensor.transpose(z0_psum[:], z_rows[:, 0, :], sort_ja[:])
        z2_f32 = keep.tile([P, P], F32)
        nc.scalar.copy(out=z2_f32[:], in_=z2_psum[:])
        z1h = keep.tile([P, N_TILES, BH], BF16)
        nc.scalar.copy(
            out=z1h[:].rearrange("x j (b h) -> x j b h", h=2),
            in_=z1_psum[:].rearrange("x (b j) -> x j b", b=RANK).unsqueeze(3).to_broadcast([P, N_TILES, RANK, 2]),
        )
        z0_sorted = keep.tile([P, P], BF16)
        nc.scalar.copy(out=z0_sorted[:], in_=z0_psum[:])

        def rows_of(source, first, n_tiles):
            return source.rearrange("x (r j) -> x j r", r=RANK)[:, first : first + n_tiles, :]

        engines = {"vector": nc.vector, "gpsimd": nc.gpsimd}

        def z1_of(who, first, n_tiles):
            if who == "vector":
                return rows_of(z1_psum[:], first, n_tiles)
            return z1h[:, first : first + n_tiles, :].rearrange("x j (b h) -> x j b h", h=2)[:, :, :, 0]

        def z0_of(source, first, n_tiles):
            return source[:, RANK * first : RANK * (first + n_tiles)].rearrange("x (j a) -> x j a", a=RANK)

        def pair_products(who, first, n_tiles):
            pair_t = work.tile([P, n_tiles, P], F32)
            z2 = rows_of(z2_f32[:], first, n_tiles)
            if who == "gpsimd":
                shape = [P, n_tiles, RANK, BH]
                nc.gpsimd.tensor_tensor(
                    out=pair_t[:].rearrange("x j (c bh) -> x j c bh", bh=BH),
                    in0=z2.unsqueeze(3).to_broadcast(shape),
                    in1=z1h[:, first : first + n_tiles, :].unsqueeze(2).to_broadcast(shape),
                    op=MULT,
                )
                return pair_t
            shape = [P, RANK, RANK, 2]
            for i in range(n_tiles):
                nc.vector.tensor_tensor(
                    out=pair_t[:, i, :].rearrange("x (c b h) -> x c b h", b=RANK, h=2),
                    in0=z2[:, i, :].unsqueeze(2).unsqueeze(3).to_broadcast(shape),
                    in1=rows_of(z1_psum[:], first + i, 1)[:, 0, :].unsqueeze(1).unsqueeze(3).to_broadcast(shape),
                    op=MULT,
                )
            return pair_t

        def next_a(first, n_tiles):
            for start, tiles in LOADS:
                if start <= first and first + n_tiles <= start + tiles:
                    return a_reps[start, tiles], (first - start) * P

        def turn(pair_t, first, n_tiles, bank):
            pair = psum.tile([P, n_tiles, P], F32, tag=bank)
            for i in range(n_tiles):
                nc.tensor.transpose(pair[:, i, :], pair_t[:, first + i, :], ident_f32[:])
            return pair

        def last_products(pair, first, n_tiles, grouped, slot):
            n = n_tiles * P
            a_rep, col = next_a(first, n_tiles)
            nc.vector.tensor_tensor(
                out=grouped[:, slot * P * PACK : (slot * P + n) * PACK].rearrange("p (n t) -> p n t", t=PACK),
                in0=pair.rearrange("p i x -> p (i x)").unsqueeze(2).to_broadcast([P, n, PACK]),
                in1=a_rep[:, :, col : col + n].rearrange("p t n -> p n t"),
                op=MULT,
            )

        def turn_words(kron_t, bank):
            turned = psum.tile([P, BANK_TILES, 2, P], F32, tag=bank)
            for i in range(BANK_TILES):
                for u in range(2):
                    nc.tensor.transpose(turned[:, i, u, :], kron_t[:, i, :].bitcast(F32)[:, u : K // 2 : 2], ident_f32[:])
            return turned

        def empty_words(engine_copy, turned, grouped, bank_tile):
            grouped_words = grouped[:].bitcast(F32).rearrange("p (j x u) -> p j x u", x=P, u=2)
            engine_copy(
                out=grouped_words[:, bank_tile : bank_tile + BANK_TILES, :, :],
                in_=turned[:].rearrange("p i u x -> p i x u"),
            )

        def quantise(grouped_cols, width):
            codes = big.tile([P, width], U32, align_bytes=64)
            scales = big.tile([P, width], U8, align_bytes=64)
            nc.vector.quantize_mx(out=codes[:].bitcast(FP8X4), scales=scales[:], in_=grouped_cols)
            return codes, scales

        def matmuls(quantised, width, banks):
            accs = []
            for half in range(OUT_ROWS // P):
                acc = psum.tile([P, width], F32, tag=banks[half])
                nc.tensor.matmul_mx(
                    out=acc[:],
                    lhsT=w_words[:, 2 * P * half : 2 * P * (half + 1)].bitcast(FP4X4),
                    lhsT_scale=w_scales[:, P * half : P * (half + 1)],
                    rhs=quantised[0][:].bitcast(FP8X4),
                    rhs_scale=quantised[1][:],
                    start=True,
                    stop=True,
                )
                accs.append(acc)
            return accs

        def matmuls_one_bank(quantised, width, bank):
            acc = psum.tile([P, OUT_ROWS // P, width], F32, tag=bank)
            for half in range(OUT_ROWS // P):
                nc.tensor.matmul_mx(
                    out=acc[:, half, :],
                    lhsT=w_words[:, 2 * P * half : 2 * P * (half + 1)].bitcast(FP4X4),
                    lhsT_scale=w_scales[:, P * half : P * (half + 1)],
                    rhs=quantised[0][:].bitcast(FP8X4),
                    rhs_scale=quantised[1][:],
                    start=True,
                    stop=True,
                )
            return acc

        def store_both(engine_copy, acc, first, width):
            result = stage.tile([P, OUT_ROWS // P, width], F32)
            engine_copy(out=result[:], in_=acc[:])
            nc.sync.dma_start(out=out.rearrange("(half p) n -> p half n", p=P)[:, :, first * P : first * P + width], in_=result[:])

        def store(engine_copy, acc, half, first, width):
            result = stage.tile([P, width], F32)
            engine_copy(out=result[:], in_=acc[:])
            nc.sync.dma_start(out=out[P * half : P * (half + 1), first * P : first * P + width], in_=result[:])

        V_COPY, S_COPY = nc.vector.tensor_copy, nc.scalar.copy

        def ba_products(first, n):
            ba_t = work.tile([P, n, RANK * RANK], F32)
            nc.vector.tensor_tensor(
                out=ba_t[:].rearrange("x j (b a) -> x j b a", a=RANK),
                in0=z1_of("gpsimd", first, n).unsqueeze(3).to_broadcast([P, n, RANK, RANK]),
                in1=z0_of(z0_psum[:], first, n).unsqueeze(2).to_broadcast([P, n, RANK, RANK]),
                op=MULT,
            )
            return ba_t

        def bc_products(who, first, n=2):
            bc_t = work.tile([P, n, RANK * RANK], F32)
            engines[who].tensor_tensor(
                out=bc_t[:].rearrange("x j (c b) -> x j c b", b=RANK),
                in0=rows_of(z2_f32[:], first, n).unsqueeze(3).to_broadcast([P, n, RANK, RANK]),
                in1=z1_of(who, first, n).unsqueeze(2).to_broadcast([P, n, RANK, RANK]),
                op=MULT,
            )
            return bc_t

        def scalar_products(kron_t, slot, ba_t, ba_slot, first, n):
            for i in range(n):
                for c in range(RANK):
                    col = c * N_TILES + first + i
                    nc.scalar.activation(
                        out=kron_t[:, slot + i, RANK * RANK * c : RANK * RANK * (c + 1)],
                        in_=ba_t[:, ba_slot + i, :],
                        func=COPY,
                        scale=z2_f32[:, col : col + 1],
                    )

        def sample_products(engine, z0_source, kron_t, slot, bc_t, bc_slot, first, parts=1):
            part = RANK * RANK // parts
            for cb in range(0, RANK * RANK, part):
                engine.tensor_tensor(
                    out=kron_t[:, slot, RANK * cb : RANK * (cb + part)].rearrange("x (cb a) -> x cb a", a=RANK),
                    in0=bc_t[:, bc_slot, cb : cb + part].unsqueeze(2).to_broadcast([P, part, RANK]),
                    in1=z0_of(z0_source, first, 1)[:, 0, :].unsqueeze(1).to_broadcast([P, part, RANK]),
                    op=MULT,
                )

        groupedV = big.tile([P, 2 * P * PACK], BF16, align_bytes=64, tag="grouped")
        grouped0 = big.tile([P, 4 * P * PACK], BF16, align_bytes=64, tag="grouped")
        groupedS = big.tile([P, 4 * P * PACK], BF16, align_bytes=64, tag="grouped")
        grouped10a = big.tile([P, 2 * P * PACK], BF16, align_bytes=64, tag="grouped")
        grouped10b = big.tile([P, 2 * P * PACK], BF16, align_bytes=64, tag="grouped")
        groupedGg = big.tile([P, 2 * P * PACK], BF16, align_bytes=64, tag="grouped")
        kron_v = big.tile([P, 2, K], BF16, tag="kron")
        kron_s0 = big.tile([P, 2, K], BF16, tag="kron")
        kron_s1 = big.tile([P, 2, K], BF16, tag="kron")
        kron_g = big.tile([P, 2, K], BF16, tag="kron")
        ba4 = ba_products(4, 3)
        scalar_products(kron_s0, 0, ba4, 0, 4, 2)
        bc7 = bc_products("vector", 7, 3)
        sample_products(nc.vector, z0_psum[:], kron_v, 0, bc7, 1, 8)
        sample_products(nc.vector, z0_psum[:], kron_v, 1, bc7, 2, 9)
        sample_products(nc.vector, z0_psum[:], kron_s1, 1, bc7, 0, 7)
        pair_t0 = pair_products("gpsimd", 0, 2)
        pair_t2 = pair_products("gpsimd", 2, 2)
        pair_t10 = pair_products("gpsimd", 10, 4)
        bc14 = bc_products("gpsimd", 14, 2)
        sample_products(nc.gpsimd, z0_sorted, kron_g, 0, bc14, 0, 14, 2)
        sample_products(nc.gpsimd, z0_sorted, kron_g, 1, bc14, 1, 15, 2)
        pair0 = turn(pair_t0, 0, 2, "b3")
        pair2 = turn(pair_t2, 0, 2, "b4")
        words_v = turn_words(kron_v, "b5")
        empty_words(S_COPY, words_v, groupedV, 0)
        scalar_products(kron_s1, 0, ba4, 2, 6, 1)
        last_products(pair0[:, 0:2, :], 0, 2, grouped0, 0)
        words_s0 = turn_words(kron_s0, "b6")
        empty_words(S_COPY, words_s0, groupedS, 0)
        pair10 = turn(pair_t10, 0, 4, "b3")
        last_products(pair2[:, 0:2, :], 2, 2, grouped0, 2)
        qV = quantise(groupedV[:], 256)
        words_s1 = turn_words(kron_s1, "b7")
        accV = matmuls_one_bank(qV, 256, "b0")
        empty_words(S_COPY, words_s1, groupedS, 2)
        store_both(S_COPY, accV, 8, 256)
        q0 = quantise(grouped0[:], 512)
        acc0 = matmuls(q0, 512, ("b1", "b5"))
        last_products(pair10[:, 0:2, :], 10, 2, grouped10a, 0)
        store(S_COPY, acc0[0], 0, 0, 512)
        store(S_COPY, acc0[1], 1, 0, 512)
        qS = quantise(groupedS[:], 512)
        words_g = turn_words(kron_g, "b7")
        empty_words(S_COPY, words_g, groupedGg, 0)
        accS = matmuls(qS, 512, ("b4", "b6"))
        store(S_COPY, accS[0], 0, 4, 512)
        store(S_COPY, accS[1], 1, 4, 512)
        q10a = quantise(grouped10a[:], 256)
        acc10a = matmuls_one_bank(q10a, 256, "b2")
        store_both(S_COPY, acc10a, 10, 256)
        last_products(pair10[:, 2:4, :], 12, 2, grouped10b, 0)
        qGg = quantise(groupedGg[:], 256)
        accGg = matmuls(qGg, 256, ("b0", "b5"))
        q10b = quantise(grouped10b[:], 256)
        store(V_COPY, accGg[0], 0, 14, 256)
        store(S_COPY, accGg[1], 1, 14, 256)
        acc10b = matmuls(q10b, 256, ("b1", "b7"))
        store(S_COPY, acc10b[0], 0, 12, 256)
        store(V_COPY, acc10b[1], 1, 12, 256)
